import numpy as np
import ml_dtypes


def mxq(x, axis, fmt="e4m3"):
    dtype, down = {"e4m3": (ml_dtypes.float8_e4m3fn, 7), "e5m2": (ml_dtypes.float8_e5m2, 14)}[fmt]
    v = np.moveaxis(np.asarray(x, np.float32).astype(ml_dtypes.bfloat16).astype(np.float64), axis, -1)
    blocks = v.reshape(v.shape[:-1] + (-1, 32))
    amax = np.abs(blocks).max(-1, keepdims=True)
    byte = np.maximum(np.where(amax > 0, np.frexp(amax)[1] - 1 + 127, 0) - down, 1)
    scale = np.exp2(byte - 127.0)
    codes = (blocks / scale).astype(np.float32).astype(dtype).astype(np.float64)
    return np.moveaxis((codes * scale).reshape(v.shape), -1, axis)


WIDE = False


def mx_kscale(k):
    if not WIDE:
        return np.ones(k)
    levels = np.array([20, -20, 10, -10, 0])
    a = np.random.permutation(np.resize(levels, k // 512 * 4)).reshape(k // 512, 4)
    idx = np.arange(k)
    return np.exp2(a[idx // 512, idx % 128 // 32])


BF16 = ml_dtypes.bfloat16


def bf(x):
    return np.asarray(x, np.float32).astype(BF16)


def f64(x):
    return np.asarray(x).astype(np.float64)


B, S, C, H, D = 4, 512, 1024, 8, 128
E = H * D
T = B * S


def rope_tables():
    inv_freq = 1.0 / (10000.0 ** (np.arange(0, D, 2) / D))
    emb = np.repeat(np.outer(np.arange(S), inv_freq), 2, axis=1)
    return np.cos(emb), np.sin(emb)


def rope(t, cos, sin):
    tr = t[..., 0::2]
    ti = t[..., 1::2]
    t_rot = np.stack([-ti, tr], axis=-1).reshape(t.shape)
    return t * cos + t_rot * sin


def rope_back(dr, cos, sin):
    u = dr * sin
    ue = u[..., 0::2]
    uo = u[..., 1::2]
    return dr * cos + np.stack([uo, -ue], axis=-1).reshape(dr.shape)


def setup_inputs():
    s = mx_kscale(T)
    cos, sin = rope_tables()
    cos, sin = bf(cos), bf(sin)
    x0 = bf(np.random.standard_normal((B, S, C)))
    Wq = bf(np.random.standard_normal((E, C)) / np.sqrt(C))
    bq = bf(np.random.standard_normal(E) * 0.1)
    g = bf(np.random.standard_normal((B, H, S, D)) * np.exp2(np.random.randint(-12, 1, (B, 1, S, 1))) / s.reshape(B, 1, S, 1))
    y = f64(x0) @ f64(Wq).T + f64(bq)
    q = y.reshape(B, S, H, D).transpose(0, 2, 1, 3)
    r = rope(q, f64(cos), f64(sin))
    return {"x": bf(f64(x0) * s.reshape(B, S, 1)), "cos": cos, "sin": sin, "Wq": Wq, "bq": bq,
            "r": np.asarray(r, np.float32), "grad_out": g}


def reference(x, cos, sin, Wq, bq, r, grad_out):
    dr = f64(grad_out) * (f64(r) > 0.0)
    dt = rope_back(dr, f64(cos), f64(sin))
    dy = dt.transpose(0, 2, 1, 3).reshape(T, E)
    xt = f64(x).reshape(T, C)
    return mxq(dy, 0, "e5m2").T @ mxq(xt, 0, "e4m3")

@@ -1,0 +1,151 @@
+from contextlib import ExitStack
+
+import concourse.mybir as mybir
+
+F32 = mybir.dt.float32
+BF16 = mybir.dt.bfloat16
+U32 = mybir.dt.uint32
+U8 = mybir.dt.uint8
+E4M3_X4 = mybir.dt.float8_e4m3fn_x4
+E5M2_X4 = mybir.dt.float8_e5m2_x4
+ALU = mybir.AluOpType
+ACT = mybir.ActivationFunctionType
+
+B, S, C, H, D = 4, 512, 1024, 8, 128
+P = 128
+PACK = 4
+PAIRS = D // 2
+N_TILE = 512
+HEAD_COLS = B * PACK * D
+
+FLOPS = 2 * B * S * H * D * C
+BYTES = 2 * (B * S * C + B * H * S * D + 2 * S * D) + 4 * (B * H * S * D + H * D * C)
+
+
+def tile_lineartransformerblock_pa_v_kernel(tc, x, cos, sin, Wq, bq, r, grad_out, out):
+    nc = tc.nc
+    with ExitStack() as stack:
+        keep = stack.enter_context(tc.tile_pool(name="keep", bufs=1))
+        loads = stack.enter_context(tc.tile_pool(name="loads", bufs=3))
+        work = stack.enter_context(tc.tile_pool(name="work", bufs=2))
+        codes = stack.enter_context(tc.tile_pool(name="codes", bufs=B + 1))
+        psum = stack.enter_context(tc.psum_pool(name="psum", bufs=4))
+
+        cos_rows = keep.tile([P, PACK, D], BF16)
+        sin_rows = keep.tile([P, PACK, PAIRS, 2], BF16)
+        nc.sync.dma_start(out=cos_rows[:], in_=cos.rearrange("(p j) d -> p j d", j=PACK))
+        nc.sync.dma_start(
+            out=sin_rows[:], in_=sin.rearrange("(p j) (i e) -> p j i e", j=PACK, e=2)
+        )
+        cos_table = keep.tile([P, D, PACK], BF16)
+        nc.vector.tensor_copy(out=cos_table[:], in_=cos_rows[:].rearrange("p j d -> p d j"))
+        cross_table = keep.tile([P, PAIRS, 2, PACK], BF16)
+        nc.vector.tensor_copy(
+            out=cross_table[:, :, 0, :], in_=sin_rows[:, :, :, 1].rearrange("p j i -> p i j")
+        )
+        nc.vector.tensor_scalar(
+            out=cross_table[:, :, 1, :],
+            in0=sin_rows[:, :, :, 0].rearrange("p j i -> p i j"),
+            scalar1=-1.0,
+            scalar2=None,
+            op0=ALU.mult,
+        )
+
+        x_codes = keep.tile([P, B, C], U32, align_bytes=64)
+        x_scales = keep.tile([P, B, C], U8, align_bytes=64)
+
+        def quantise_x(b):
+            x_rows = loads.tile([P, PACK, C], BF16, bufs=2)
+            nc.sync.dma_start(out=x_rows[:], in_=x[b].rearrange("(p j) c -> p j c", j=PACK))
+            x_grouped = work.tile([P, C, PACK], BF16, align_bytes=64)
+            for n in range(C // N_TILE):
+                cols = slice(n * N_TILE, (n + 1) * N_TILE)
+                nc.scalar.copy(
+                    out=x_grouped[:, cols, :].rearrange("p (c i) j -> p c j i", i=4),
+                    in_=x_rows[:, :, cols].rearrange("p j (c i) -> p c j i", i=4),
+                )
+            nc.vector.quantize_mx(
+                out=x_codes[:, b, :].bitcast(E4M3_X4),
+                scales=x_scales[:, b, :],
+                in_=x_grouped[:].rearrange("p c j -> p (c j)"),
+            )
+
+        def quantise_dy(h):
+            r_rows = loads.tile([P, B, PACK * D], F32)
+            g_rows = loads.tile([P, B, PACK * D], BF16)
+            nc.sync.dma_start(
+                out=r_rows[:], in_=r[:, h].rearrange("b (p j) d -> p b (j d)", j=PACK)
+            )
+            nc.sync.dma_start(
+                out=g_rows[:], in_=grad_out[:, h].rearrange("b (p j) d -> p b (j d)", j=PACK)
+            )
+            r_sign = work.tile([P, HEAD_COLS], BF16)
+            mask = work.tile([P, HEAD_COLS], BF16)
+            nc.scalar.activation(
+                out=r_sign[:], in_=r_rows[:].rearrange("p b f -> p (b f)"), func=ACT.Sign
+            )
+            nc.scalar.activation(out=mask[:], in_=r_sign[:], func=ACT.Relu)
+            dr = work.tile([P, B, PACK, PAIRS, 2], BF16)
+            nc.vector.tensor_tensor(
+                out=dr[:].rearrange("p b j i e -> p (b j i e)"),
+                in0=mask[:],
+                in1=g_rows[:].rearrange("p b f -> p (b f)"),
+                op=ALU.mult,
+            )
+            own = work.tile([P, B, D, PACK], F32)
+            nc.vector.tensor_tensor(
+                out=own[:],
+                in0=dr[:].rearrange("p b j i e -> p b (i e) j"),
+                in1=cos_table[:].unsqueeze(1).to_broadcast([P, B, D, PACK]),
+                op=ALU.mult,
+            )
+            cross = work.tile([P, B, PAIRS, 2, PACK], F32)
+            for e in range(2):
+                nc.vector.tensor_tensor(
+                    out=cross[:, :, :, e, :],
+                    in0=dr[:, :, :, :, 1 - e].rearrange("p b j i -> p b i j"),
+                    in1=cross_table[:, :, e, :].unsqueeze(1).to_broadcast([P, B, PAIRS, PACK]),
+                    op=ALU.mult,
+                )
+            dy_grouped = work.tile([P, HEAD_COLS], BF16, align_bytes=64)
+            nc.vector.tensor_tensor(
+                out=dy_grouped[:],
+                in0=own[:].rearrange("p b d j -> p (b d j)"),
+                in1=cross[:].rearrange("p b i e j -> p (b i e j)"),
+                op=ALU.add,
+            )
+            dy_codes = codes.tile([P, B * D], U32, align_bytes=64)
+            dy_scales = codes.tile([P, B * D], U8, align_bytes=64)
+            nc.vector.quantize_mx(
+                out=dy_codes[:].bitcast(E5M2_X4), scales=dy_scales[:], in_=dy_grouped[:]
+            )
+            return dy_codes, dy_scales
+
+        def multiply(h, dy_codes, dy_scales):
+            out_rows = work.tile([P, C], F32, bufs=3)
+            for n in range(C // N_TILE):
+                cols = slice(n * N_TILE, (n + 1) * N_TILE)
+                acc = psum.tile([P, N_TILE], F32)
+                for b in range(B):
+                    head_cols = slice(b * D, (b + 1) * D)
+                    nc.tensor.matmul_mx(
+                        out=acc[:],
+                        lhsT=dy_codes[:, head_cols].bitcast(E5M2_X4),
+                        lhsT_scale=dy_scales[:, head_cols],
+                        rhs=x_codes[:, b, cols].bitcast(E4M3_X4),
+                        rhs_scale=x_scales[:, b, cols],
+                        start=(b == 0),
+                        stop=(b == B - 1),
+                    )
+                nc.scalar.copy(out=out_rows[:, cols], in_=acc[:])
+            nc.scalar.dma_start(out=out[h * D : (h + 1) * D, :], in_=out_rows[:])
+
+        waiting = []
+        for h in range(H):
+            waiting.append((h, quantise_dy(h)))
+            if h < B:
+                quantise_x(h)
+            if h >= B - 1:
+                for k, (dy_codes, dy_scales) in waiting:
+                    multiply(k, dy_codes, dy_scales)
+                waiting = []

@@ -16,7 +16,10 @@ P = 128
 PACK = 4
 PAIRS = D // 2
 N_TILE = 512
-HEAD_COLS = B * PACK * D
+N_BANKS = C // N_TILE
+NB = 2
+ROWS = 2 * NB
+RUN = 4
 
 FLOPS = 2 * B * S * H * D * C
 BYTES = 2 * (B * S * C + B * H * S * D + 2 * S * D) + 4 * (B * H * S * D + H * D * C)
@@ -28,27 +31,16 @@ def tile_lineartransformerblock_pa_v_kernel(tc, x, cos, sin, Wq, bq, r, grad_out
         keep = stack.enter_context(tc.tile_pool(name="keep", bufs=1))
         loads = stack.enter_context(tc.tile_pool(name="loads", bufs=3))
         work = stack.enter_context(tc.tile_pool(name="work", bufs=2))
-        codes = stack.enter_context(tc.tile_pool(name="codes", bufs=B + 1))
-        psum = stack.enter_context(tc.psum_pool(name="psum", bufs=4))
+        codes = stack.enter_context(tc.tile_pool(name="codes", bufs=6))
+        psum = stack.enter_context(tc.psum_pool(name="psum", bufs=8))
 
-        cos_rows = keep.tile([P, PACK, D], BF16)
+        cos_rows = keep.tile([P, PACK, PAIRS, 2], BF16)
         sin_rows = keep.tile([P, PACK, PAIRS, 2], BF16)
-        nc.sync.dma_start(out=cos_rows[:], in_=cos.rearrange("(p j) d -> p j d", j=PACK))
+        nc.sync.dma_start(
+            out=cos_rows[:], in_=cos.rearrange("(p j) (i e) -> p j i e", j=PACK, e=2)
+        )
         nc.sync.dma_start(
             out=sin_rows[:], in_=sin.rearrange("(p j) (i e) -> p j i e", j=PACK, e=2)
-        )
-        cos_table = keep.tile([P, D, PACK], BF16)
-        nc.vector.tensor_copy(out=cos_table[:], in_=cos_rows[:].rearrange("p j d -> p d j"))
-        cross_table = keep.tile([P, PAIRS, 2, PACK], BF16)
-        nc.vector.tensor_copy(
-            out=cross_table[:, :, 0, :], in_=sin_rows[:, :, :, 1].rearrange("p j i -> p i j")
-        )
-        nc.vector.tensor_scalar(
-            out=cross_table[:, :, 1, :],
-            in0=sin_rows[:, :, :, 0].rearrange("p j i -> p i j"),
-            scalar1=-1.0,
-            scalar2=None,
-            op0=ALU.mult,
         )
 
         x_codes = keep.tile([P, B, C], U32, align_bytes=64)
@@ -58,11 +50,11 @@ def tile_lineartransformerblock_pa_v_kernel(tc, x, cos, sin, Wq, bq, r, grad_out
             x_rows = loads.tile([P, PACK, C], BF16, bufs=2)
             nc.sync.dma_start(out=x_rows[:], in_=x[b].rearrange("(p j) c -> p j c", j=PACK))
             x_grouped = work.tile([P, C, PACK], BF16, align_bytes=64)
-            for n in range(C // N_TILE):
+            for n in range(N_BANKS):
                 cols = slice(n * N_TILE, (n + 1) * N_TILE)
                 nc.scalar.copy(
-                    out=x_grouped[:, cols, :].rearrange("p (c i) j -> p c j i", i=4),
-                    in_=x_rows[:, :, cols].rearrange("p j (c i) -> p c j i", i=4),
+                    out=x_grouped[:, cols, :].rearrange("p (c i) j -> p c j i", i=RUN),
+                    in_=x_rows[:, :, cols].rearrange("p j (c i) -> p c j i", i=RUN),
                 )
             nc.vector.quantize_mx(
                 out=x_codes[:, b, :].bitcast(E4M3_X4),
@@ -70,82 +62,109 @@ def tile_lineartransformerblock_pa_v_kernel(tc, x, cos, sin, Wq, bq, r, grad_out
                 in_=x_grouped[:].rearrange("p c j -> p (c j)"),
             )
 
-        def quantise_dy(h):
-            r_rows = loads.tile([P, B, PACK * D], F32)
-            g_rows = loads.tile([P, B, PACK * D], BF16)
-            nc.sync.dma_start(
-                out=r_rows[:], in_=r[:, h].rearrange("b (p j) d -> p b (j d)", j=PACK)
-            )
-            nc.sync.dma_start(
-                out=g_rows[:], in_=grad_out[:, h].rearrange("b (p j) d -> p b (j d)", j=PACK)
-            )
-            r_sign = work.tile([P, HEAD_COLS], BF16)
-            mask = work.tile([P, HEAD_COLS], BF16)
+        def quantise_dy(g, first_batch, dy_codes, dy_scales):
+            r_rows = loads.tile([P, NB, 2, PACK * D], F32)
+            g_rows = loads.tile([P, NB, 2, PACK * D], BF16)
+            batches = slice(first_batch, first_batch + NB)
+            for k in range(2):
+                nc.sync.dma_start(
+                    out=r_rows[:, :, k, :],
+                    in_=r[batches, 2 * g + k].rearrange("b (p j) d -> p b (j d)", j=PACK),
+                )
+                nc.sync.dma_start(
+                    out=g_rows[:, :, k, :],
+                    in_=grad_out[batches, 2 * g + k].rearrange("b (p j) d -> p b (j d)", j=PACK),
+                )
+            r_sign = work.tile([P, ROWS * PACK * D], BF16)
+            mask = work.tile([P, ROWS, PACK, D], BF16)
             nc.scalar.activation(
-                out=r_sign[:], in_=r_rows[:].rearrange("p b f -> p (b f)"), func=ACT.Sign
+                out=r_sign[:], in_=r_rows[:].rearrange("p b k f -> p (b k f)"), func=ACT.Sign
             )
-            nc.scalar.activation(out=mask[:], in_=r_sign[:], func=ACT.Relu)
-            dr = work.tile([P, B, PACK, PAIRS, 2], BF16)
+            nc.scalar.activation(
+                out=mask[:].rearrange("p q j d -> p (q j d)"), in_=r_sign[:], func=ACT.Relu
+            )
+            dr = work.tile([P, PACK, ROWS, PAIRS, 2], BF16)
             nc.vector.tensor_tensor(
-                out=dr[:].rearrange("p b j i e -> p (b j i e)"),
+                out=dr[:].rearrange("p j q i e -> p q j (i e)"),
                 in0=mask[:],
-                in1=g_rows[:].rearrange("p b f -> p (b f)"),
+                in1=g_rows[:].rearrange("p b k (j d) -> p (b k) j d", j=PACK),
                 op=ALU.mult,
             )
-            own = work.tile([P, B, D, PACK], F32)
-            nc.vector.tensor_tensor(
-                out=own[:],
-                in0=dr[:].rearrange("p b j i e -> p b (i e) j"),
-                in1=cos_table[:].unsqueeze(1).to_broadcast([P, B, D, PACK]),
-                op=ALU.mult,
-            )
-            cross = work.tile([P, B, PAIRS, 2, PACK], F32)
-            for e in range(2):
+            for parity in range(2):
+                own = work.tile([P, PACK, ROWS, PAIRS], F32)
                 nc.vector.tensor_tensor(
-                    out=cross[:, :, :, e, :],
-                    in0=dr[:, :, :, :, 1 - e].rearrange("p b j i -> p b i j"),
-                    in1=cross_table[:, :, e, :].unsqueeze(1).to_broadcast([P, B, PAIRS, PACK]),
+                    out=own[:],
+                    in0=dr[:, :, :, :, parity],
+                    in1=cos_rows[:, :, :, parity].unsqueeze(2).to_broadcast([P, PACK, ROWS, PAIRS]),
                     op=ALU.mult,
                 )
-            dy_grouped = work.tile([P, HEAD_COLS], BF16, align_bytes=64)
-            nc.vector.tensor_tensor(
-                out=dy_grouped[:],
-                in0=own[:].rearrange("p b d j -> p (b d j)"),
-                in1=cross[:].rearrange("p b i e j -> p (b i e j)"),
-                op=ALU.add,
-            )
-            dy_codes = codes.tile([P, B * D], U32, align_bytes=64)
-            dy_scales = codes.tile([P, B * D], U8, align_bytes=64)
-            nc.vector.quantize_mx(
-                out=dy_codes[:].bitcast(E5M2_X4), scales=dy_scales[:], in_=dy_grouped[:]
-            )
-            return dy_codes, dy_scales
+                partner = work.tile([P, PACK, ROWS, PAIRS], F32)
+                nc.vector.tensor_tensor(
+                    out=partner[:],
+                    in0=dr[:, :, :, :, 1 - parity],
+                    in1=sin_rows[:, :, :, 1 - parity]
+                    .unsqueeze(2)
+                    .to_broadcast([P, PACK, ROWS, PAIRS]),
+                    op=ALU.mult,
+                )
+                dy_grouped = work.tile([P, ROWS * PAIRS, PACK], BF16, align_bytes=64)
+                nc.vector.tensor_tensor(
+                    out=dy_grouped[:].rearrange("p (c i) j -> p c j i", i=RUN),
+                    in0=own[:].rearrange("p j q (c i) -> p (q c) j i", i=RUN),
+                    in1=partner[:].rearrange("p j q (c i) -> p (q c) j i", i=RUN),
+                    op=(ALU.add if parity == 0 else ALU.subtract),
+                )
+                piece_cols = slice(first_batch * P, (first_batch + NB) * P)
+                nc.vector.quantize_mx(
+                    out=dy_codes[parity][:, piece_cols].bitcast(E5M2_X4),
+                    scales=dy_scales[parity][:, piece_cols],
+                    in_=dy_grouped[:].rearrange("p c j -> p (c j)"),
+                )
 
-        def multiply(h, dy_codes, dy_scales):
-            out_rows = work.tile([P, C], F32, bufs=3)
-            for n in range(C // N_TILE):
-                cols = slice(n * N_TILE, (n + 1) * N_TILE)
-                acc = psum.tile([P, N_TILE], F32)
-                for b in range(B):
-                    head_cols = slice(b * D, (b + 1) * D)
-                    nc.tensor.matmul_mx(
-                        out=acc[:],
-                        lhsT=dy_codes[:, head_cols].bitcast(E5M2_X4),
-                        lhsT_scale=dy_scales[:, head_cols],
-                        rhs=x_codes[:, b, cols].bitcast(E4M3_X4),
-                        rhs_scale=x_scales[:, b, cols],
-                        start=(b == 0),
-                        stop=(b == B - 1),
+        def multiply(first_batch, dy_codes, dy_scales, acc):
+            for parity in range(2):
+                for n in range(N_BANKS):
+                    for b in range(first_batch, first_batch + NB):
+                        nc.tensor.matmul_mx(
+                            out=acc[parity][n][:],
+                            lhsT=dy_codes[parity][:, b * P : (b + 1) * P].bitcast(E5M2_X4),
+                            lhsT_scale=dy_scales[parity][:, b * P : (b + 1) * P],
+                            rhs=x_codes[:, b, n * N_TILE : (n + 1) * N_TILE].bitcast(E4M3_X4),
+                            rhs_scale=x_scales[:, b, n * N_TILE : (n + 1) * N_TILE],
+                            start=(b == 0),
+                            stop=(b == B - 1),
+                        )
+
+        def store(g, acc):
+            out_blocks = out.rearrange("(g m e) c -> g e m c", m=P, e=2)
+            for parity in range(2):
+                out_rows = work.tile([P, C], F32, bufs=3)
+                for n in range(N_BANKS):
+                    nc.scalar.copy(
+                        out=out_rows[:, n * N_TILE : (n + 1) * N_TILE], in_=acc[parity][n][:]
                     )
-                nc.scalar.copy(out=out_rows[:, cols], in_=acc[:])
-            nc.scalar.dma_start(out=out[h * D : (h + 1) * D, :], in_=out_rows[:])
+                nc.scalar.dma_start(out=out_blocks[g, parity], in_=out_rows[:])
 
+        x_done = 0
         waiting = []
-        for h in range(H):
-            waiting.append((h, quantise_dy(h)))
-            if h < B:
-                quantise_x(h)
-            if h >= B - 1:
-                for k, (dy_codes, dy_scales) in waiting:
-                    multiply(k, dy_codes, dy_scales)
-                waiting = []
+        for g in range(H // 2):
+            dy_codes = [codes.tile([P, B * P], U32, align_bytes=64, name="dy_codes") for e in range(2)]
+            dy_scales = [codes.tile([P, B * P], U8, align_bytes=64, name="dy_scales") for e in range(2)]
+            acc = [
+                [psum.tile([P, N_TILE], F32, name="acc") for n in range(N_BANKS)] for e in range(2)
+            ]
+            for first_batch in range(0, B, NB):
+                quantise_dy(g, first_batch, dy_codes, dy_scales)
+                waiting.append((g, first_batch, dy_codes, dy_scales, acc))
+                if x_done < B:
+                    quantise_x(x_done)
+                    x_done += 1
+                still_waiting = []
+                for piece in waiting:
+                    if piece[1] + NB <= x_done:
+                        multiply(piece[1], piece[2], piece[3], piece[4])
+                        if piece[1] + NB == B:
+                            store(piece[0], piece[4])
+                    else:
+                        still_waiting.append(piece)
+                waiting = still_waiting

@@ -20,6 +20,7 @@ N_BANKS = C // N_TILE
 NB = 2
 ROWS = 2 * NB
 RUN = 4
+LEAD = 2
 
 FLOPS = 2 * B * S * H * D * C
 BYTES = 2 * (B * S * C + B * H * S * D + 2 * S * D) + 4 * (B * H * S * D + H * D * C)
@@ -29,19 +30,22 @@ def tile_lineartransformerblock_pa_v_kernel(tc, x, cos, sin, Wq, bq, r, grad_out
     nc = tc.nc
     with ExitStack() as stack:
         keep = stack.enter_context(tc.tile_pool(name="keep", bufs=1))
-        loads = stack.enter_context(tc.tile_pool(name="loads", bufs=3))
+        loads = stack.enter_context(tc.tile_pool(name="loads", bufs=LEAD + 2))
         work = stack.enter_context(tc.tile_pool(name="work", bufs=2))
-        codes = stack.enter_context(tc.tile_pool(name="codes", bufs=6))
+        codes = stack.enter_context(tc.tile_pool(name="codes", bufs=H))
         psum = stack.enter_context(tc.psum_pool(name="psum", bufs=8))
 
-        cos_rows = keep.tile([P, PACK, PAIRS, 2], BF16)
-        sin_rows = keep.tile([P, PACK, PAIRS, 2], BF16)
-        nc.sync.dma_start(
-            out=cos_rows[:], in_=cos.rearrange("(p j) (i e) -> p j i e", j=PACK, e=2)
-        )
-        nc.sync.dma_start(
-            out=sin_rows[:], in_=sin.rearrange("(p j) (i e) -> p j i e", j=PACK, e=2)
-        )
+        def load_piece(g, first_batch):
+            r_rows = loads.tile([P, NB, 2, PACK * D], F32)
+            g_rows = loads.tile([P, NB, 2, PACK * D], BF16)
+            batches = slice(first_batch, first_batch + NB)
+            for rows, source in ((r_rows, r), (g_rows, grad_out)):
+                for k in range(2):
+                    nc.sync.dma_start(
+                        out=rows[:, :, k, :],
+                        in_=source[batches, 2 * g + k].rearrange("b (p j) d -> p b (j d)", j=PACK),
+                    )
+            return r_rows, g_rows
 
         x_codes = keep.tile([P, B, C], U32, align_bytes=64)
         x_scales = keep.tile([P, B, C], U8, align_bytes=64)
@@ -62,27 +66,27 @@ def tile_lineartransformerblock_pa_v_kernel(tc, x, cos, sin, Wq, bq, r, grad_out
                 in_=x_grouped[:].rearrange("p c j -> p (c j)"),
             )
 
-        def quantise_dy(g, first_batch, dy_codes, dy_scales):
-            r_rows = loads.tile([P, NB, 2, PACK * D], F32)
-            g_rows = loads.tile([P, NB, 2, PACK * D], BF16)
-            batches = slice(first_batch, first_batch + NB)
-            for k in range(2):
-                nc.sync.dma_start(
-                    out=r_rows[:, :, k, :],
-                    in_=r[batches, 2 * g + k].rearrange("b (p j) d -> p b (j d)", j=PACK),
+        def relu_mask(r_rows, on_vector):
+            mask = work.tile([P, ROWS, PACK, D], BF16, bufs=LEAD + 1)
+            if on_vector:
+                nc.vector.tensor_scalar(
+                    out=mask[:].rearrange("p q j d -> p (q j d)"),
+                    in0=r_rows[:].rearrange("p b k f -> p (b k f)"),
+                    scalar1=0.0,
+                    scalar2=None,
+                    op0=ALU.is_gt,
                 )
-                nc.sync.dma_start(
-                    out=g_rows[:, :, k, :],
-                    in_=grad_out[batches, 2 * g + k].rearrange("b (p j) d -> p b (j d)", j=PACK),
+            else:
+                r_sign = work.tile([P, ROWS * PACK * D], BF16)
+                nc.scalar.activation(
+                    out=r_sign[:], in_=r_rows[:].rearrange("p b k f -> p (b k f)"), func=ACT.Sign
                 )
-            r_sign = work.tile([P, ROWS * PACK * D], BF16)
-            mask = work.tile([P, ROWS, PACK, D], BF16)
-            nc.scalar.activation(
-                out=r_sign[:], in_=r_rows[:].rearrange("p b k f -> p (b k f)"), func=ACT.Sign
-            )
-            nc.scalar.activation(
-                out=mask[:].rearrange("p q j d -> p (q j d)"), in_=r_sign[:], func=ACT.Relu
-            )
+                nc.scalar.activation(
+                    out=mask[:].rearrange("p q j d -> p (q j d)"), in_=r_sign[:], func=ACT.Relu
+                )
+            return mask
+
+        def quantise_dy(first_batch, mask, g_rows, dy_codes, dy_scales):
             dr = work.tile([P, PACK, ROWS, PAIRS, 2], BF16)
             nc.vector.tensor_tensor(
                 out=dr[:].rearrange("p j q i e -> p q j (i e)"),
@@ -138,33 +142,61 @@ def tile_lineartransformerblock_pa_v_kernel(tc, x, cos, sin, Wq, bq, r, grad_out
         def store(g, acc):
             out_blocks = out.rearrange("(g m e) c -> g e m c", m=P, e=2)
             for parity in range(2):
-                out_rows = work.tile([P, C], F32, bufs=3)
                 for n in range(N_BANKS):
-                    nc.scalar.copy(
-                        out=out_rows[:, n * N_TILE : (n + 1) * N_TILE], in_=acc[parity][n][:]
+                    out_rows = work.tile([P, N_TILE], F32, bufs=4)
+                    nc.scalar.copy(out=out_rows[:], in_=acc[parity][n][:])
+                    nc.scalar.dma_start(
+                        out=out_blocks[g, parity][:, n * N_TILE : (n + 1) * N_TILE], in_=out_rows[:]
                     )
-                nc.scalar.dma_start(out=out_blocks[g, parity], in_=out_rows[:])
+
+        pieces = [(g, first_batch) for g in range(H // 2) for first_batch in range(0, B, NB)]
+        prepared = []
+
+        def prepare(step):
+            r_rows, g_rows = load_piece(pieces[step][0], pieces[step][1])
+            prepared.append((relu_mask(r_rows, on_vector=(step == 0)), g_rows))
+
+        prepare(0)
+
+        cos_rows = keep.tile([P, PACK, PAIRS, 2], BF16)
+        sin_rows = keep.tile([P, PACK, PAIRS, 2], BF16)
+        nc.sync.dma_start(
+            out=cos_rows[:], in_=cos.rearrange("(p j) (i e) -> p j i e", j=PACK, e=2)
+        )
+        nc.sync.dma_start(
+            out=sin_rows[:], in_=sin.rearrange("(p j) (i e) -> p j i e", j=PACK, e=2)
+        )
+        for step in range(1, LEAD):
+            prepare(step)
 
         x_done = 0
         waiting = []
-        for g in range(H // 2):
-            dy_codes = [codes.tile([P, B * P], U32, align_bytes=64, name="dy_codes") for e in range(2)]
-            dy_scales = [codes.tile([P, B * P], U8, align_bytes=64, name="dy_scales") for e in range(2)]
-            acc = [
-                [psum.tile([P, N_TILE], F32, name="acc") for n in range(N_BANKS)] for e in range(2)
-            ]
-            for first_batch in range(0, B, NB):
-                quantise_dy(g, first_batch, dy_codes, dy_scales)
-                waiting.append((g, first_batch, dy_codes, dy_scales, acc))
-                if x_done < B:
-                    quantise_x(x_done)
-                    x_done += 1
-                still_waiting = []
-                for piece in waiting:
-                    if piece[1] + NB <= x_done:
-                        multiply(piece[1], piece[2], piece[3], piece[4])
-                        if piece[1] + NB == B:
-                            store(piece[0], piece[4])
-                    else:
-                        still_waiting.append(piece)
-                waiting = still_waiting
+        for step, (g, first_batch) in enumerate(pieces):
+            if step + LEAD < len(pieces):
+                prepare(step + LEAD)
+            if first_batch == 0:
+                dy_codes = [
+                    codes.tile([P, B * P], U32, align_bytes=64, name="dy_codes") for e in range(2)
+                ]
+                dy_scales = [
+                    codes.tile([P, B * P], U8, align_bytes=64, name="dy_scales") for e in range(2)
+                ]
+                acc = [
+                    [psum.tile([P, N_TILE], F32, name="acc") for n in range(N_BANKS)]
+                    for e in range(2)
+                ]
+            mask, g_rows = prepared[step]
+            quantise_dy(first_batch, mask, g_rows, dy_codes, dy_scales)
+            waiting.append((g, first_batch, dy_codes, dy_scales, acc))
+            if x_done < B:
+                quantise_x(x_done)
+                x_done += 1
+            still_waiting = []
+            for piece in waiting:
+                if not still_waiting and piece[1] + NB <= x_done:
+                    multiply(piece[1], piece[2], piece[3], piece[4])
+                    if piece[1] + NB == B:
+                        store(piece[0], piece[4])
+                else:
+                    still_waiting.append(piece)
+            waiting = still_waiting

@@ -1,6 +1,7 @@
 from contextlib import ExitStack
 
 import concourse.mybir as mybir
+from concourse.masks import make_identity
 
 F32 = mybir.dt.float32
 BF16 = mybir.dt.bfloat16
@@ -21,6 +22,7 @@ NB = 2
 ROWS = 2 * NB
 RUN = 4
 LEAD = 2
+VECTOR_MASKS = 2
 
 FLOPS = 2 * B * S * H * D * C
 BYTES = 2 * (B * S * C + B * H * S * D + 2 * S * D) + 4 * (B * H * S * D + H * D * C)
@@ -33,7 +35,9 @@ def tile_lineartransformerblock_pa_v_kernel(tc, x, cos, sin, Wq, bq, r, grad_out
         loads = stack.enter_context(tc.tile_pool(name="loads", bufs=LEAD + 2))
         work = stack.enter_context(tc.tile_pool(name="work", bufs=2))
         codes = stack.enter_context(tc.tile_pool(name="codes", bufs=H))
-        psum = stack.enter_context(tc.psum_pool(name="psum", bufs=8))
+        table_banks = stack.enter_context(tc.psum_pool(name="table_banks", bufs=1))
+        psum = stack.enter_context(tc.psum_pool(name="psum", bufs=6))
+        stack.enter_context(tc.manual_schedule())
 
         def load_piece(g, first_batch):
             r_rows = loads.tile([P, NB, 2, PACK * D], F32)
@@ -47,28 +51,9 @@ def tile_lineartransformerblock_pa_v_kernel(tc, x, cos, sin, Wq, bq, r, grad_out
                     )
             return r_rows, g_rows
 
-        x_codes = keep.tile([P, B, C], U32, align_bytes=64)
-        x_scales = keep.tile([P, B, C], U8, align_bytes=64)
-
-        def quantise_x(b):
-            x_rows = loads.tile([P, PACK, C], BF16, bufs=2)
-            nc.sync.dma_start(out=x_rows[:], in_=x[b].rearrange("(p j) c -> p j c", j=PACK))
-            x_grouped = work.tile([P, C, PACK], BF16, align_bytes=64)
-            for n in range(N_BANKS):
-                cols = slice(n * N_TILE, (n + 1) * N_TILE)
-                nc.scalar.copy(
-                    out=x_grouped[:, cols, :].rearrange("p (c i) j -> p c j i", i=RUN),
-                    in_=x_rows[:, :, cols].rearrange("p j (c i) -> p c j i", i=RUN),
-                )
-            nc.vector.quantize_mx(
-                out=x_codes[:, b, :].bitcast(E4M3_X4),
-                scales=x_scales[:, b, :],
-                in_=x_grouped[:].rearrange("p c j -> p (c j)"),
-            )
-
         def relu_mask(r_rows, on_vector):
-            mask = work.tile([P, ROWS, PACK, D], BF16, bufs=LEAD + 1)
             if on_vector:
+                mask = work.tile([P, ROWS, PACK, D], BF16, name="vector_mask")
                 nc.vector.tensor_scalar(
                     out=mask[:].rearrange("p q j d -> p (q j d)"),
                     in0=r_rows[:].rearrange("p b k f -> p (b k f)"),
@@ -77,6 +62,7 @@ def tile_lineartransformerblock_pa_v_kernel(tc, x, cos, sin, Wq, bq, r, grad_out
                     op0=ALU.is_gt,
                 )
             else:
+                mask = work.tile([P, ROWS, PACK, D], BF16, name="scalar_mask", bufs=LEAD + 1)
                 r_sign = work.tile([P, ROWS * PACK * D], BF16)
                 nc.scalar.activation(
                     out=r_sign[:], in_=r_rows[:].rearrange("p b k f -> p (b k f)"), func=ACT.Sign
@@ -86,7 +72,32 @@ def tile_lineartransformerblock_pa_v_kernel(tc, x, cos, sin, Wq, bq, r, grad_out
                 )
             return mask
 
-        def quantise_dy(first_batch, mask, g_rows, dy_codes, dy_scales):
+        x_codes = keep.tile([P, B, C], U32, align_bytes=64)
+        x_scales = keep.tile([P, B, C], U8, align_bytes=64)
+
+        def load_x(b):
+            x_rows = loads.tile([P, PACK, C], BF16, bufs=2)
+            nc.sync.dma_start(out=x_rows[:], in_=x[b].rearrange("(p j) c -> p j c", j=PACK))
+            return x_rows
+
+        def regroup_x(x_rows):
+            x_grouped = work.tile([P, C, PACK], BF16, align_bytes=64)
+            for n in range(N_BANKS):
+                cols = slice(n * N_TILE, (n + 1) * N_TILE)
+                nc.scalar.copy(
+                    out=x_grouped[:, cols, :].rearrange("p (c i) j -> p c j i", i=RUN),
+                    in_=x_rows[:, :, cols].rearrange("p j (c i) -> p c j i", i=RUN),
+                )
+            return x_grouped
+
+        def quantise_x(b, x_grouped):
+            nc.vector.quantize_mx(
+                out=x_codes[:, b, :].bitcast(E4M3_X4),
+                scales=x_scales[:, b, :],
+                in_=x_grouped[:].rearrange("p c j -> p (c j)"),
+            )
+
+        def relu_backward(mask, g_rows):
             dr = work.tile([P, PACK, ROWS, PAIRS, 2], BF16)
             nc.vector.tensor_tensor(
                 out=dr[:].rearrange("p j q i e -> p q j (i e)"),
@@ -94,36 +105,45 @@ def tile_lineartransformerblock_pa_v_kernel(tc, x, cos, sin, Wq, bq, r, grad_out
                 in1=g_rows[:].rearrange("p b k (j d) -> p (b k) j d", j=PACK),
                 op=ALU.mult,
             )
+            return dr
+
+        def rope_products(dr):
+            products = []
             for parity in range(2):
-                own = work.tile([P, PACK, ROWS, PAIRS], F32)
-                nc.vector.tensor_tensor(
-                    out=own[:],
-                    in0=dr[:, :, :, :, parity],
-                    in1=cos_rows[:, :, :, parity].unsqueeze(2).to_broadcast([P, PACK, ROWS, PAIRS]),
-                    op=ALU.mult,
-                )
-                partner = work.tile([P, PACK, ROWS, PAIRS], F32)
-                nc.vector.tensor_tensor(
-                    out=partner[:],
-                    in0=dr[:, :, :, :, 1 - parity],
-                    in1=sin_rows[:, :, :, 1 - parity]
-                    .unsqueeze(2)
-                    .to_broadcast([P, PACK, ROWS, PAIRS]),
-                    op=ALU.mult,
-                )
-                dy_grouped = work.tile([P, ROWS * PAIRS, PACK], BF16, align_bytes=64)
-                nc.vector.tensor_tensor(
-                    out=dy_grouped[:].rearrange("p (c i) j -> p c j i", i=RUN),
-                    in0=own[:].rearrange("p j q (c i) -> p (q c) j i", i=RUN),
-                    in1=partner[:].rearrange("p j q (c i) -> p (q c) j i", i=RUN),
-                    op=(ALU.add if parity == 0 else ALU.subtract),
-                )
-                piece_cols = slice(first_batch * P, (first_batch + NB) * P)
-                nc.vector.quantize_mx(
-                    out=dy_codes[parity][:, piece_cols].bitcast(E5M2_X4),
-                    scales=dy_scales[parity][:, piece_cols],
-                    in_=dy_grouped[:].rearrange("p c j -> p (c j)"),
-                )
+                own = work.tile([P, PACK, ROWS, PAIRS], F32, bufs=3)
+                partner = work.tile([P, PACK, ROWS, PAIRS], F32, bufs=3)
+                for product, channel, table in (
+                    (own, parity, cos_planes),
+                    (partner, 1 - parity, sin_planes),
+                ):
+                    nc.vector.tensor_tensor(
+                        out=product[:],
+                        in0=dr[:, :, :, :, channel],
+                        in1=table[:, channel].unsqueeze(2).to_broadcast([P, PACK, ROWS, PAIRS]),
+                        op=ALU.mult,
+                    )
+                products.append((own, partner))
+            return products
+
+        def combine(engine, parity, own, partner):
+            dy_grouped = work.tile(
+                [P, ROWS * PAIRS, PACK], BF16, align_bytes=64, name="dy_grouped_%d" % parity
+            )
+            engine.tensor_tensor(
+                out=dy_grouped[:].rearrange("p (c i) j -> p c j i", i=RUN),
+                in0=own[:].rearrange("p j q (c i) -> p (q c) j i", i=RUN),
+                in1=partner[:].rearrange("p j q (c i) -> p (q c) j i", i=RUN),
+                op=(ALU.add if parity == 0 else ALU.subtract),
+            )
+            return dy_grouped
+
+        def quantise_plane(first_batch, plane_codes, plane_scales, dy_grouped):
+            piece_cols = slice(first_batch * P, (first_batch + NB) * P)
+            nc.vector.quantize_mx(
+                out=plane_codes[:, piece_cols].bitcast(E5M2_X4),
+                scales=plane_scales[:, piece_cols],
+                in_=dy_grouped[:].rearrange("p c j -> p (c j)"),
+            )
 
         def multiply(first_batch, dy_codes, dy_scales, acc):
             for parity in range(2):
@@ -150,53 +170,95 @@ def tile_lineartransformerblock_pa_v_kernel(tc, x, cos, sin, Wq, bq, r, grad_out
                     )
 
         pieces = [(g, first_batch) for g in range(H // 2) for first_batch in range(0, B, NB)]
-        prepared = []
+        n_pieces = len(pieces)
+        loaded = {}
+        mask_of = {}
+        x_rows = {}
+        x_grouped = {}
 
-        def prepare(step):
-            r_rows, g_rows = load_piece(pieces[step][0], pieces[step][1])
-            prepared.append((relu_mask(r_rows, on_vector=(step == 0)), g_rows))
+        def get_ready(step):
+            loaded[step] = load_piece(pieces[step][0], pieces[step][1])
+            if step >= VECTOR_MASKS:
+                mask_of[step] = relu_mask(loaded[step][0], on_vector=False)
 
-        prepare(0)
+        identity = keep.tile([P, P], BF16)
+        make_identity(nc, identity[:])
+        get_ready(0)
 
-        cos_rows = keep.tile([P, PACK, PAIRS, 2], BF16)
-        sin_rows = keep.tile([P, PACK, PAIRS, 2], BF16)
-        nc.sync.dma_start(
-            out=cos_rows[:], in_=cos.rearrange("(p j) (i e) -> p j i e", j=PACK, e=2)
-        )
-        nc.sync.dma_start(
-            out=sin_rows[:], in_=sin.rearrange("(p j) (i e) -> p j i e", j=PACK, e=2)
-        )
+        cos_planes = table_banks.tile([P, 2, PACK, PAIRS], F32)
+        sin_planes = table_banks.tile([P, 2, PACK, PAIRS], F32)
+        for planes, source in ((cos_planes, cos), (sin_planes, sin)):
+            table_rows = keep.tile([P, PACK, PAIRS, 2], BF16, name="table_rows", bufs=2)
+            nc.sync.dma_start(
+                out=table_rows[:], in_=source.rearrange("(p j) (i e) -> p j i e", j=PACK, e=2)
+            )
+            for parity in range(2):
+                nc.tensor.matmul(
+                    out=planes[:, parity].rearrange("p j i -> p (j i)"),
+                    lhsT=identity[:],
+                    rhs=table_rows[:, :, :, parity].rearrange("p j i -> p (j i)"),
+                    start=True,
+                    stop=True,
+                )
+        x_rows[0] = load_x(0)
         for step in range(1, LEAD):
-            prepare(step)
+            get_ready(step)
 
-        x_done = 0
         waiting = []
-        for step, (g, first_batch) in enumerate(pieces):
-            if step + LEAD < len(pieces):
-                prepare(step + LEAD)
-            if first_batch == 0:
-                dy_codes = [
-                    codes.tile([P, B * P], U32, align_bytes=64, name="dy_codes") for e in range(2)
-                ]
-                dy_scales = [
-                    codes.tile([P, B * P], U8, align_bytes=64, name="dy_scales") for e in range(2)
-                ]
-                acc = [
-                    [psum.tile([P, N_TILE], F32, name="acc") for n in range(N_BANKS)]
-                    for e in range(2)
-                ]
-            mask, g_rows = prepared[step]
-            quantise_dy(first_batch, mask, g_rows, dy_codes, dy_scales)
-            waiting.append((g, first_batch, dy_codes, dy_scales, acc))
-            if x_done < B:
-                quantise_x(x_done)
-                x_done += 1
+        finished = []
+        acc_of = {}
+        codes_of = {}
+        planes_of = {}
+        x_done = 0
+        for step in range(n_pieces + 2):
+            if step < B:
+                x_grouped[step] = regroup_x(x_rows[step])
+            if step + 1 < B:
+                x_rows[step + 1] = load_x(step + 1)
+            if step + LEAD < n_pieces:
+                get_ready(step + LEAD)
+            for g in finished:
+                store(g, acc_of[g])
+            finished = []
+
+            if step < n_pieces:
+                if step < VECTOR_MASKS:
+                    mask_of[step] = relu_mask(loaded[step][0], on_vector=True)
+                dr = relu_backward(mask_of[step], loaded[step][1])
+            if 0 < step <= n_pieces:
+                g, first_batch = pieces[step - 1]
+                quantise_plane(first_batch, codes_of[g][0][0], codes_of[g][1][0], planes_of[step - 1][0])
+            if step < n_pieces:
+                products = rope_products(dr)
+            if 0 < step <= n_pieces:
+                quantise_plane(first_batch, codes_of[g][0][1], codes_of[g][1][1], planes_of[step - 1][1])
+                waiting.append((g, first_batch))
+            if 0 < step <= B:
+                quantise_x(step - 1, x_grouped[step - 1])
+                x_done = step
+            if step < n_pieces:
+                if pieces[step][1] == 0:
+                    codes_of[pieces[step][0]] = (
+                        [codes.tile([P, B * P], U32, align_bytes=64, name="dy_codes") for e in range(2)],
+                        [codes.tile([P, B * P], U8, align_bytes=64, name="dy_scales") for e in range(2)],
+                    )
+                odd_engine = nc.gpsimd if step + 1 < n_pieces else nc.vector
+                planes_of[step] = (
+                    combine(nc.vector, 0, products[0][0], products[0][1]),
+                    combine(odd_engine, 1, products[1][0], products[1][1]),
+                )
+
             still_waiting = []
-            for piece in waiting:
-                if not still_waiting and piece[1] + NB <= x_done:
-                    multiply(piece[1], piece[2], piece[3], piece[4])
-                    if piece[1] + NB == B:
-                        store(piece[0], piece[4])
+            for g, first_batch in waiting:
+                if not still_waiting and first_batch + NB <= x_done:
+                    if first_batch == 0:
+                        acc_of[g] = [
+                            [psum.tile([P, N_TILE], F32, name="acc") for n in range(N_BANKS)]
+                            for e in range(2)
+                        ]
+                    multiply(first_batch, codes_of[g][0], codes_of[g][1], acc_of[g])
+                    if first_batch + NB == B:
+                        finished.append(g)
                 else:
-                    still_waiting.append(piece)
+                    still_waiting.append((g, first_batch))
             waiting = still_waiting

@@ -21,6 +21,7 @@ N_BANKS = C // N_TILE
 NB = 2
 ROWS = 2 * NB
 RUN = 4
+GPSIMD_RUN = 1
 LEAD = 2
 VECTOR_MASKS = 2
 
@@ -109,30 +110,25 @@ def tile_lineartransformerblock_pa_v_kernel(tc, x, cos, sin, Wq, bq, r, grad_out
 
         def rope_products(dr):
             products = []
-            for parity in range(2):
-                own = work.tile([P, PACK, ROWS, PAIRS], F32, bufs=3)
-                partner = work.tile([P, PACK, ROWS, PAIRS], F32, bufs=3)
-                for product, channel, table in (
-                    (own, parity, cos_planes),
-                    (partner, 1 - parity, sin_planes),
-                ):
-                    nc.vector.tensor_tensor(
-                        out=product[:],
-                        in0=dr[:, :, :, :, channel],
-                        in1=table[:, channel].unsqueeze(2).to_broadcast([P, PACK, ROWS, PAIRS]),
-                        op=ALU.mult,
-                    )
-                products.append((own, partner))
+            for channel in range(2):
+                both = work.tile([P, 2, PACK, ROWS, PAIRS], F32, bufs=4)
+                nc.vector.tensor_tensor(
+                    out=both[:],
+                    in0=dr[:, :, :, :, channel].unsqueeze(1).to_broadcast([P, 2, PACK, ROWS, PAIRS]),
+                    in1=table_planes[channel][:].unsqueeze(3).to_broadcast([P, 2, PACK, ROWS, PAIRS]),
+                    op=ALU.mult,
+                )
+                products.append(both)
             return products
 
-        def combine(engine, parity, own, partner):
+        def combine(engine, run, parity, products):
             dy_grouped = work.tile(
                 [P, ROWS * PAIRS, PACK], BF16, align_bytes=64, name="dy_grouped_%d" % parity
             )
             engine.tensor_tensor(
-                out=dy_grouped[:].rearrange("p (c i) j -> p c j i", i=RUN),
-                in0=own[:].rearrange("p j q (c i) -> p (q c) j i", i=RUN),
-                in1=partner[:].rearrange("p j q (c i) -> p (q c) j i", i=RUN),
+                out=dy_grouped[:].rearrange("p (c i) j -> p c j i", i=run),
+                in0=products[parity][:, 0].rearrange("p j q (c i) -> p (q c) j i", i=run),
+                in1=products[1 - parity][:, 1].rearrange("p j q (c i) -> p (q c) j i", i=run),
                 op=(ALU.add if parity == 0 else ALU.subtract),
             )
             return dy_grouped
@@ -185,18 +181,19 @@ def tile_lineartransformerblock_pa_v_kernel(tc, x, cos, sin, Wq, bq, r, grad_out
         make_identity(nc, identity[:])
         get_ready(0)
 
-        cos_planes = table_banks.tile([P, 2, PACK, PAIRS], F32)
-        sin_planes = table_banks.tile([P, 2, PACK, PAIRS], F32)
-        for planes, source in ((cos_planes, cos), (sin_planes, sin)):
+        table_planes = [
+            table_banks.tile([P, 2, PACK, PAIRS], F32, name="table_planes_%d" % e) for e in range(2)
+        ]
+        for t, source in enumerate((cos, sin)):
             table_rows = keep.tile([P, PACK, PAIRS, 2], BF16, name="table_rows", bufs=2)
             nc.sync.dma_start(
                 out=table_rows[:], in_=source.rearrange("(p j) (i e) -> p j i e", j=PACK, e=2)
             )
-            for parity in range(2):
+            for channel in range(2):
                 nc.tensor.matmul(
-                    out=planes[:, parity].rearrange("p j i -> p (j i)"),
+                    out=table_planes[channel][:, t].rearrange("p j i -> p (j i)"),
                     lhsT=identity[:],
-                    rhs=table_rows[:, :, :, parity].rearrange("p j i -> p (j i)"),
+                    rhs=table_rows[:, :, :, channel].rearrange("p j i -> p (j i)"),
                     start=True,
                     stop=True,
                 )
@@ -208,7 +205,8 @@ def tile_lineartransformerblock_pa_v_kernel(tc, x, cos, sin, Wq, bq, r, grad_out
         finished = []
         acc_of = {}
         codes_of = {}
-        planes_of = {}
+        products_of = {}
+        even_planes = {}
         x_done = 0
         for step in range(n_pieces + 2):
             if step < B:
@@ -227,11 +225,15 @@ def tile_lineartransformerblock_pa_v_kernel(tc, x, cos, sin, Wq, bq, r, grad_out
                 dr = relu_backward(mask_of[step], loaded[step][1])
             if 0 < step <= n_pieces:
                 g, first_batch = pieces[step - 1]
-                quantise_plane(first_batch, codes_of[g][0][0], codes_of[g][1][0], planes_of[step - 1][0])
+                quantise_plane(first_batch, codes_of[g][0][0], codes_of[g][1][0], even_planes[step - 1])
+                if step < n_pieces:
+                    odd_plane = combine(nc.gpsimd, GPSIMD_RUN, 1, products_of[step - 1])
+                else:
+                    odd_plane = combine(nc.vector, RUN, 1, products_of[step - 1])
             if step < n_pieces:
-                products = rope_products(dr)
+                products_of[step] = rope_products(dr)
             if 0 < step <= n_pieces:
-                quantise_plane(first_batch, codes_of[g][0][1], codes_of[g][1][1], planes_of[step - 1][1])
+                quantise_plane(first_batch, codes_of[g][0][1], codes_of[g][1][1], odd_plane)
                 waiting.append((g, first_batch))
             if 0 < step <= B:
                 quantise_x(step - 1, x_grouped[step - 1])
@@ -242,11 +244,7 @@ def tile_lineartransformerblock_pa_v_kernel(tc, x, cos, sin, Wq, bq, r, grad_out
                         [codes.tile([P, B * P], U32, align_bytes=64, name="dy_codes") for e in range(2)],
                         [codes.tile([P, B * P], U8, align_bytes=64, name="dy_scales") for e in range(2)],
                     )
-                odd_engine = nc.gpsimd if step + 1 < n_pieces else nc.vector
-                planes_of[step] = (
-                    combine(nc.vector, 0, products[0][0], products[0][1]),
-                    combine(odd_engine, 1, products[1][0], products[1][1]),
-                )
+                even_planes[step] = combine(nc.vector, RUN, 0, products_of[step])
 
             still_waiting = []
             for g, first_batch in waiting:

@@ -21,7 +21,6 @@ N_BANKS = C // N_TILE
 NB = 2
 ROWS = 2 * NB
 RUN = 4
-GPSIMD_RUN = 1
 LEAD = 2
 VECTOR_MASKS = 2
 
@@ -121,14 +120,14 @@ def tile_lineartransformerblock_pa_v_kernel(tc, x, cos, sin, Wq, bq, r, grad_out
                 products.append(both)
             return products
 
-        def combine(engine, run, parity, products):
+        def combine(engine, parity, products):
             dy_grouped = work.tile(
                 [P, ROWS * PAIRS, PACK], BF16, align_bytes=64, name="dy_grouped_%d" % parity
             )
             engine.tensor_tensor(
-                out=dy_grouped[:].rearrange("p (c i) j -> p c j i", i=run),
-                in0=products[parity][:, 0].rearrange("p j q (c i) -> p (q c) j i", i=run),
-                in1=products[1 - parity][:, 1].rearrange("p j q (c i) -> p (q c) j i", i=run),
+                out=dy_grouped[:].rearrange("p (c i) j -> p c j i", i=RUN),
+                in0=products[parity][:, 0].rearrange("p j q (c i) -> p (q c) j i", i=RUN),
+                in1=products[1 - parity][:, 1].rearrange("p j q (c i) -> p (q c) j i", i=RUN),
                 op=(ALU.add if parity == 0 else ALU.subtract),
             )
             return dy_grouped
@@ -227,9 +226,9 @@ def tile_lineartransformerblock_pa_v_kernel(tc, x, cos, sin, Wq, bq, r, grad_out
                 g, first_batch = pieces[step - 1]
                 quantise_plane(first_batch, codes_of[g][0][0], codes_of[g][1][0], even_planes[step - 1])
                 if step < n_pieces:
-                    odd_plane = combine(nc.gpsimd, GPSIMD_RUN, 1, products_of[step - 1])
+                    odd_plane = combine(nc.gpsimd, 1, products_of[step - 1])
                 else:
-                    odd_plane = combine(nc.vector, RUN, 1, products_of[step - 1])
+                    odd_plane = combine(nc.vector, 1, products_of[step - 1])
             if step < n_pieces:
                 products_of[step] = rope_products(dr)
             if 0 < step <= n_pieces:
@@ -244,7 +243,7 @@ def tile_lineartransformerblock_pa_v_kernel(tc, x, cos, sin, Wq, bq, r, grad_out
                         [codes.tile([P, B * P], U32, align_bytes=64, name="dy_codes") for e in range(2)],
                         [codes.tile([P, B * P], U8, align_bytes=64, name="dy_scales") for e in range(2)],
                     )
-                even_planes[step] = combine(nc.vector, RUN, 0, products_of[step])
+                even_planes[step] = combine(nc.vector, 0, products_of[step])
 
             still_waiting = []
             for g, first_batch in waiting:

@@ -19,10 +19,15 @@ PAIRS = D // 2
 N_TILE = 512
 N_BANKS = C // N_TILE
 NB = 2
-ROWS = 2 * NB
 RUN = 4
-LEAD = 2
-VECTOR_MASKS = 2
+V_MASKS = 99
+X_AHEAD = 0
+X_RATE = 1
+MX_LAG = 3
+MX_EXTRA = 3
+V_PRODUCTS = 3
+SPLIT_FIRST = 1
+SPLIT_LAST = 1
 
 FLOPS = 2 * B * S * H * D * C
 BYTES = 2 * (B * S * C + B * H * S * D + 2 * S * D) + 4 * (B * H * S * D + H * D * C)
@@ -32,230 +37,236 @@ def tile_lineartransformerblock_pa_v_kernel(tc, x, cos, sin, Wq, bq, r, grad_out
     nc = tc.nc
     with ExitStack() as stack:
         keep = stack.enter_context(tc.tile_pool(name="keep", bufs=1))
-        loads = stack.enter_context(tc.tile_pool(name="loads", bufs=LEAD + 2))
-        work = stack.enter_context(tc.tile_pool(name="work", bufs=2))
-        codes = stack.enter_context(tc.tile_pool(name="codes", bufs=H))
-        table_banks = stack.enter_context(tc.psum_pool(name="table_banks", bufs=1))
-        psum = stack.enter_context(tc.psum_pool(name="psum", bufs=6))
+        loads = stack.enter_context(tc.tile_pool(name="loads", bufs=6))
+        work = stack.enter_context(tc.tile_pool(name="work", bufs=3))
+        psum = stack.enter_context(tc.psum_pool(name="psum", bufs=3))
         stack.enter_context(tc.manual_schedule())
 
-        def load_piece(g, first_batch):
-            r_rows = loads.tile([P, NB, 2, PACK * D], F32)
-            g_rows = loads.tile([P, NB, 2, PACK * D], BF16)
-            batches = slice(first_batch, first_batch + NB)
+        pieces = []
+        for h in range(H):
+            for first in range(0, B, NB):
+                if (h == 0 and first == 0 and SPLIT_FIRST) or (h == H - 1 and first == B - NB and SPLIT_LAST):
+                    pieces += [(h, first + k, 1) for k in range(NB)]
+                else:
+                    pieces.append((h, first, NB))
+        n_pieces = len(pieces)
+
+        def load_piece(q):
+            h, first, nb = pieces[q]
+            r_rows = loads.tile([P, nb, PACK * D], F32, name="r_rows")
+            g_rows = loads.tile([P, nb, PACK * D], BF16, name="g_rows")
             for rows, source in ((r_rows, r), (g_rows, grad_out)):
-                for k in range(2):
-                    nc.sync.dma_start(
-                        out=rows[:, :, k, :],
-                        in_=source[batches, 2 * g + k].rearrange("b (p j) d -> p b (j d)", j=PACK),
-                    )
+                nc.sync.dma_start(
+                    out=rows[:],
+                    in_=source[first : first + nb, h].rearrange("b (p j) d -> p b (j d)", j=PACK),
+                )
             return r_rows, g_rows
 
-        def relu_mask(r_rows, on_vector):
-            if on_vector:
-                mask = work.tile([P, ROWS, PACK, D], BF16, name="vector_mask")
-                nc.vector.tensor_scalar(
-                    out=mask[:].rearrange("p q j d -> p (q j d)"),
-                    in0=r_rows[:].rearrange("p b k f -> p (b k f)"),
-                    scalar1=0.0,
-                    scalar2=None,
-                    op0=ALU.is_gt,
-                )
-            else:
-                mask = work.tile([P, ROWS, PACK, D], BF16, name="scalar_mask", bufs=LEAD + 1)
-                r_sign = work.tile([P, ROWS * PACK * D], BF16)
-                nc.scalar.activation(
-                    out=r_sign[:], in_=r_rows[:].rearrange("p b k f -> p (b k f)"), func=ACT.Sign
-                )
-                nc.scalar.activation(
-                    out=mask[:].rearrange("p q j d -> p (q j d)"), in_=r_sign[:], func=ACT.Relu
-                )
-            return mask
-
-        x_codes = keep.tile([P, B, C], U32, align_bytes=64)
-        x_scales = keep.tile([P, B, C], U8, align_bytes=64)
-
-        def load_x(b):
-            x_rows = loads.tile([P, PACK, C], BF16, bufs=2)
-            nc.sync.dma_start(out=x_rows[:], in_=x[b].rearrange("(p j) c -> p j c", j=PACK))
+        def load_x(chunk):
+            n, b = divmod(chunk, B)
+            x_rows = loads.tile([P, PACK, N_TILE], BF16, name="x_rows", bufs=4)
+            nc.sync.dma_start(
+                out=x_rows[:],
+                in_=x[b].rearrange("(p j) c -> p j c", j=PACK)[:, :, n * N_TILE : (n + 1) * N_TILE],
+            )
             return x_rows
 
-        def regroup_x(x_rows):
-            x_grouped = work.tile([P, C, PACK], BF16, align_bytes=64)
-            for n in range(N_BANKS):
-                cols = slice(n * N_TILE, (n + 1) * N_TILE)
-                nc.scalar.copy(
-                    out=x_grouped[:, cols, :].rearrange("p (c i) j -> p c j i", i=RUN),
-                    in_=x_rows[:, :, cols].rearrange("p j (c i) -> p c j i", i=RUN),
-                )
-            return x_grouped
+        def relu_mask(q):
+            r_rows = loaded[q][0]
+            n_cols = pieces[q][2] * PACK * D
+            mask = work.tile([P, n_cols], BF16, name="mask")
+            flat = r_rows[:].rearrange("p b f -> p (b f)")
+            if q < V_MASKS:
+                nc.vector.tensor_scalar(out=mask[:], in0=flat, scalar1=0.0, scalar2=None, op0=ALU.is_gt)
+            else:
+                r_sign = work.tile([P, n_cols], BF16, name="r_sign")
+                nc.scalar.activation(out=r_sign[:], in_=flat, func=ACT.Sign)
+                nc.scalar.activation(out=mask[:], in_=r_sign[:], func=ACT.Relu)
+            return mask
 
-        def quantise_x(b, x_grouped):
-            nc.vector.quantize_mx(
-                out=x_codes[:, b, :].bitcast(E4M3_X4),
-                scales=x_scales[:, b, :],
-                in_=x_grouped[:].rearrange("p c j -> p (c j)"),
-            )
-
-        def relu_backward(mask, g_rows):
-            dr = work.tile([P, PACK, ROWS, PAIRS, 2], BF16)
-            nc.vector.tensor_tensor(
-                out=dr[:].rearrange("p j q i e -> p q j (i e)"),
-                in0=mask[:],
-                in1=g_rows[:].rearrange("p b k (j d) -> p (b k) j d", j=PACK),
+        def relu_backward(q):
+            dr = work.tile([P, pieces[q][2] * PACK * D], BF16, name="dr")
+            engine = nc.vector if q < V_PRODUCTS else nc.gpsimd
+            engine.tensor_tensor(
+                out=dr[:],
+                in0=mask_of[q][:],
+                in1=loaded[q][1][:].rearrange("p b f -> p (b f)"),
                 op=ALU.mult,
             )
             return dr
 
-        def rope_products(dr):
-            products = []
-            for channel in range(2):
-                both = work.tile([P, 2, PACK, ROWS, PAIRS], F32, bufs=4)
+        def turn(words):
+            n_blocks = words.shape[1] // P
+            turned = psum.tile([P, n_blocks, P], F32, name="turned")
+            for k in range(n_blocks):
+                nc.tensor.transpose(turned[:, k, :], words[:, k * P : (k + 1) * P], ident_f[:])
+            return turned
+
+        def rope_products(q, turned):
+            nb = pieces[q][2]
+            products = work.tile([P, 2, nb, 2, 2, P], F32, name="products")
+            for t in range(2):
                 nc.vector.tensor_tensor(
-                    out=both[:],
-                    in0=dr[:, :, :, :, channel].unsqueeze(1).to_broadcast([P, 2, PACK, ROWS, PAIRS]),
-                    in1=table_planes[channel][:].unsqueeze(3).to_broadcast([P, 2, PACK, ROWS, PAIRS]),
+                    out=products[:, t],
+                    in0=turned[:].bitcast(BF16).rearrange("w (b k) (p e) -> w b k e p", k=2, e=2),
+                    in1=tables[:, t].unsqueeze(1).to_broadcast([P, nb, 2, 2, P]),
                     op=ALU.mult,
                 )
-                products.append(both)
             return products
 
-        def combine(engine, parity, products):
-            dy_grouped = work.tile(
-                [P, ROWS * PAIRS, PACK], BF16, align_bytes=64, name="dy_grouped_%d" % parity
-            )
-            engine.tensor_tensor(
-                out=dy_grouped[:].rearrange("p (c i) j -> p c j i", i=RUN),
-                in0=products[parity][:, 0].rearrange("p j q (c i) -> p (q c) j i", i=RUN),
-                in1=products[1 - parity][:, 1].rearrange("p j q (c i) -> p (q c) j i", i=RUN),
-                op=(ALU.add if parity == 0 else ALU.subtract),
-            )
-            return dy_grouped
-
-        def quantise_plane(first_batch, plane_codes, plane_scales, dy_grouped):
-            piece_cols = slice(first_batch * P, (first_batch + NB) * P)
-            nc.vector.quantize_mx(
-                out=plane_codes[:, piece_cols].bitcast(E5M2_X4),
-                scales=plane_scales[:, piece_cols],
-                in_=dy_grouped[:].rearrange("p c j -> p (c j)"),
-            )
-
-        def multiply(first_batch, dy_codes, dy_scales, acc):
-            for parity in range(2):
-                for n in range(N_BANKS):
-                    for b in range(first_batch, first_batch + NB):
-                        nc.tensor.matmul_mx(
-                            out=acc[parity][n][:],
-                            lhsT=dy_codes[parity][:, b * P : (b + 1) * P].bitcast(E5M2_X4),
-                            lhsT_scale=dy_scales[parity][:, b * P : (b + 1) * P],
-                            rhs=x_codes[:, b, n * N_TILE : (n + 1) * N_TILE].bitcast(E4M3_X4),
-                            rhs_scale=x_scales[:, b, n * N_TILE : (n + 1) * N_TILE],
-                            start=(b == 0),
-                            stop=(b == B - 1),
+        def add_back(products, b):
+            summed = psum.tile([P, 2, PACK * PAIRS], F32, name="summed")
+            for e in range(2):
+                for jj in range(2):
+                    for t in range(2):
+                        nc.tensor.matmul(
+                            out=summed[:, e, jj * P : (jj + 1) * P],
+                            lhsT=products[:, t, b, jj, e if t == 0 else 1 - e, :],
+                            rhs=ident_f[:],
+                            start=(t == 0),
+                            stop=(t == 1),
+                            is_transpose=True,
                         )
+            return summed
 
-        def store(g, acc):
-            out_blocks = out.rearrange("(g m e) c -> g e m c", m=P, e=2)
-            for parity in range(2):
-                for n in range(N_BANKS):
-                    out_rows = work.tile([P, N_TILE], F32, bufs=4)
-                    nc.scalar.copy(out=out_rows[:], in_=acc[parity][n][:])
-                    nc.scalar.dma_start(
-                        out=out_blocks[g, parity][:, n * N_TILE : (n + 1) * N_TILE], in_=out_rows[:]
-                    )
+        def quantise_piece(q, dy_grouped):
+            nb = pieces[q][2]
+            dy_codes = keep.tile([P, nb * D], U32, align_bytes=64, name="dy_codes_%d" % q)
+            dy_scales = keep.tile([P, nb * D], U8, align_bytes=64, name="dy_scales_%d" % q)
+            nc.vector.quantize_mx(
+                out=dy_codes[:].bitcast(E5M2_X4),
+                scales=dy_scales[:],
+                in_=dy_grouped[:].rearrange("p b d j -> p (b d j)"),
+            )
+            for k in range(nb):
+                cols = slice(k * D, (k + 1) * D)
+                codes_of[(pieces[q][0], pieces[q][1] + k)] = (dy_codes[:, cols], dy_scales[:, cols])
 
-        pieces = [(g, first_batch) for g in range(H // 2) for first_batch in range(0, B, NB)]
-        n_pieces = len(pieces)
+        x_codes = keep.tile([P, B, C], U32, align_bytes=64)
+        x_scales = keep.tile([P, B, C], U8, align_bytes=64)
+
+        def regroup_x(chunk):
+            x_grouped = work.tile([P, N_TILE, PACK], BF16, align_bytes=64, name="x_grouped")
+            nc.scalar.copy(
+                out=x_grouped[:].rearrange("p (c i) j -> p c j i", i=RUN),
+                in_=x_rows[chunk][:].rearrange("p j (c i) -> p c j i", i=RUN),
+            )
+            return x_grouped
+
+        def quantise_x(chunk):
+            n, b = divmod(chunk, B)
+            cols = slice(n * N_TILE, (n + 1) * N_TILE)
+            nc.vector.quantize_mx(
+                out=x_codes[:, b, cols].bitcast(E4M3_X4),
+                scales=x_scales[:, b, cols],
+                in_=x_grouped_of[chunk][:].rearrange("p c j -> p (c j)"),
+            )
+
+        def multiply(h, n):
+            acc = psum.tile([P, N_TILE], F32, name="acc", bufs=2)
+            for b in range(B):
+                dy_codes, dy_scales = codes_of[(h, b)]
+                nc.tensor.matmul_mx(
+                    out=acc[:],
+                    lhsT=dy_codes.bitcast(E5M2_X4),
+                    lhsT_scale=dy_scales,
+                    rhs=x_codes[:, b, n * N_TILE : (n + 1) * N_TILE].bitcast(E4M3_X4),
+                    rhs_scale=x_scales[:, b, n * N_TILE : (n + 1) * N_TILE],
+                    start=(b == 0),
+                    stop=(b == B - 1),
+                )
+            return acc
+
+        def store(h, n, acc):
+            out_rows = work.tile([P, N_TILE], F32, name="out_rows", bufs=4)
+            nc.scalar.copy(out=out_rows[:], in_=acc[:])
+            nc.scalar.dma_start(
+                out=out[h * D : (h + 1) * D, n * N_TILE : (n + 1) * N_TILE], in_=out_rows[:]
+            )
+
         loaded = {}
         mask_of = {}
+        dr_of = {}
+        turned_of = {}
+        products_of = {}
+        grouped_of = {}
+        codes_of = {}
         x_rows = {}
-        x_grouped = {}
+        x_grouped_of = {}
 
-        def get_ready(step):
-            loaded[step] = load_piece(pieces[step][0], pieces[step][1])
-            if step >= VECTOR_MASKS:
-                mask_of[step] = relu_mask(loaded[step][0], on_vector=False)
+        load_order = [("r", 0), ("r", 1)]
+        for k in range(max(n_pieces - 2, B * N_BANKS)):
+            if k < B * N_BANKS:
+                load_order.append(("x", k))
+            if k + 2 < n_pieces:
+                load_order.append(("r", k + 2))
 
-        identity = keep.tile([P, P], BF16)
-        make_identity(nc, identity[:])
-        get_ready(0)
-
-        table_planes = [
-            table_banks.tile([P, 2, PACK, PAIRS], F32, name="table_planes_%d" % e) for e in range(2)
-        ]
+        table_rows = keep.tile([P, 2, PACK * D], BF16, name="table_rows")
         for t, source in enumerate((cos, sin)):
-            table_rows = keep.tile([P, PACK, PAIRS, 2], BF16, name="table_rows", bufs=2)
-            nc.sync.dma_start(
-                out=table_rows[:], in_=source.rearrange("(p j) (i e) -> p j i e", j=PACK, e=2)
-            )
-            for channel in range(2):
-                nc.tensor.matmul(
-                    out=table_planes[channel][:, t].rearrange("p j i -> p (j i)"),
-                    lhsT=identity[:],
-                    rhs=table_rows[:, :, :, channel].rearrange("p j i -> p (j i)"),
-                    start=True,
-                    stop=True,
-                )
-        x_rows[0] = load_x(0)
-        for step in range(1, LEAD):
-            get_ready(step)
+            nc.sync.dma_start(out=table_rows[:, t], in_=source.rearrange("(p j) d -> p (j d)", j=PACK))
+
+        def issue(count):
+            for kind, k in load_order[:count]:
+                if kind == "r":
+                    loaded[k] = load_piece(k)
+                else:
+                    x_rows[k] = load_x(k)
+            return load_order[count:]
+
+        load_order = issue(5)
+
+        ident_f = keep.tile([P, P], F32, name="ident_f")
+        make_identity(nc, ident_f[:])
+
+        tables = keep.tile([P, 2, 2, 2, P], BF16, name="tables")
+        sin_even = table_rows[:, 1].rearrange("p (q e) -> p q e", e=2)[:, :, 0]
+        nc.vector.tensor_scalar(out=sin_even, in0=sin_even, scalar1=-1.0, scalar2=None, op0=ALU.mult)
+        turned_tables = turn(table_rows[:].rearrange("p t f -> p (t f)").bitcast(F32))
+        table_source = turned_tables[:].bitcast(BF16).rearrange("w (t k) (p e) -> w t k e p", t=2, e=2)
+        for t in range(2):
+            nc.scalar.copy(out=tables[:, t], in_=table_source[:, t])
 
         waiting = []
         finished = []
-        acc_of = {}
-        codes_of = {}
-        products_of = {}
-        even_planes = {}
         x_done = 0
-        for step in range(n_pieces + 2):
-            if step < B:
-                x_grouped[step] = regroup_x(x_rows[step])
-            if step + 1 < B:
-                x_rows[step + 1] = load_x(step + 1)
-            if step + LEAD < n_pieces:
-                get_ready(step + LEAD)
-            for g in finished:
-                store(g, acc_of[g])
+        for step in range(-2, n_pieces + 9):
+            load_order = issue(2)
+            for h, n, acc in finished:
+                store(h, n, acc)
             finished = []
-
-            if step < n_pieces:
-                if step < VECTOR_MASKS:
-                    mask_of[step] = relu_mask(loaded[step][0], on_vector=True)
-                dr = relu_backward(mask_of[step], loaded[step][1])
-            if 0 < step <= n_pieces:
-                g, first_batch = pieces[step - 1]
-                quantise_plane(first_batch, codes_of[g][0][0], codes_of[g][1][0], even_planes[step - 1])
-                if step < n_pieces:
-                    odd_plane = combine(nc.gpsimd, 1, products_of[step - 1])
-                else:
-                    odd_plane = combine(nc.vector, 1, products_of[step - 1])
-            if step < n_pieces:
-                products_of[step] = rope_products(dr)
-            if 0 < step <= n_pieces:
-                quantise_plane(first_batch, codes_of[g][0][1], codes_of[g][1][1], odd_plane)
-                waiting.append((g, first_batch))
-            if 0 < step <= B:
-                quantise_x(step - 1, x_grouped[step - 1])
-                x_done = step
-            if step < n_pieces:
-                if pieces[step][1] == 0:
-                    codes_of[pieces[step][0]] = (
-                        [codes.tile([P, B * P], U32, align_bytes=64, name="dy_codes") for e in range(2)],
-                        [codes.tile([P, B * P], U8, align_bytes=64, name="dy_scales") for e in range(2)],
+            if V_MASKS <= step + 3 < n_pieces:
+                mask_of[step + 3] = relu_mask(step + 3)
+            for chunk in range(X_RATE * step + X_AHEAD, X_RATE * (step + 1) + X_AHEAD):
+                if 0 <= chunk < B * N_BANKS:
+                    x_grouped_of[chunk] = regroup_x(chunk)
+            if 0 <= step < n_pieces:
+                products_of[step] = rope_products(step, turned_of[step])
+            if 0 <= step - 1 < n_pieces:
+                q = step - 1
+                grouped_of[q] = work.tile([P, pieces[q][2], D, PACK], BF16, align_bytes=64, name="dy_grouped")
+                for b in range(pieces[q][2]):
+                    summed = add_back(products_of[q], b)
+                    nc.scalar.copy(
+                        out=grouped_of[q][:, b].rearrange("p (i e) j -> p i e j", e=2),
+                        in_=summed[:].rearrange("p e (j i) -> p i e j", j=PACK),
                     )
-                even_planes[step] = combine(nc.vector, 0, products_of[step])
-
-            still_waiting = []
-            for g, first_batch in waiting:
-                if not still_waiting and first_batch + NB <= x_done:
-                    if first_batch == 0:
-                        acc_of[g] = [
-                            [psum.tile([P, N_TILE], F32, name="acc") for n in range(N_BANKS)]
-                            for e in range(2)
-                        ]
-                    multiply(first_batch, codes_of[g][0], codes_of[g][1], acc_of[g])
-                    if first_batch + NB == B:
-                        finished.append(g)
-                else:
-                    still_waiting.append((g, first_batch))
-            waiting = still_waiting
+            if 0 <= step - 2 < n_pieces:
+                quantise_piece(step - 2, grouped_of[step - 2])
+            for chunk in range(X_RATE * (step - 1) + X_AHEAD, X_RATE * step + X_AHEAD):
+                if 0 <= chunk < B * N_BANKS:
+                    quantise_x(chunk)
+                    x_done = chunk + 1
+            if 0 <= step + 2 < n_pieces:
+                if step + 2 < V_MASKS:
+                    mask_of[step + 2] = relu_mask(step + 2)
+                dr_of[step + 2] = relu_backward(step + 2)
+            q = step - MX_LAG
+            if 0 <= q < n_pieces and pieces[q][1] + pieces[q][2] == B:
+                waiting += [(pieces[q][0], n) for n in range(N_BANKS)]
+            limit = 2 if step % MX_EXTRA == 0 or step > n_pieces else 1
+            ready = [(h, n) for h, n in waiting if x_done >= (n + 1) * B][:limit]
+            for h, n in ready:
+                waiting.remove((h, n))
+                finished.append((h, n, multiply(h, n)))
+            if 0 <= step + 1 < n_pieces:
+                turned_of[step + 1] = turn(dr_of[step + 1][:].bitcast(F32))

@@ -15,7 +15,6 @@ ACT = mybir.ActivationFunctionType
 B, S, C, H, D = 4, 512, 1024, 8, 128
 P = 128
 PACK = 4
-PAIRS = D // 2
 N_TILE = 512
 N_BANKS = C // N_TILE
 NB = 2
@@ -95,38 +94,37 @@ def tile_lineartransformerblock_pa_v_kernel(tc, x, cos, sin, Wq, bq, r, grad_out
             )
             return dr
 
-        def turn(words):
-            n_blocks = words.shape[1] // P
-            turned = psum.tile([P, n_blocks, P], F32, name="turned")
+        def turn(rows):
+            n_blocks = rows.shape[1] // P
+            turned = psum.tile([P, n_blocks * P], BF16, name="turned")
             for k in range(n_blocks):
-                nc.tensor.transpose(turned[:, k, :], words[:, k * P : (k + 1) * P], ident_f[:])
+                cols = slice(k * P, (k + 1) * P)
+                nc.tensor.transpose(turned[:, cols], rows[:, cols], ident_bf[:])
             return turned
 
         def rope_products(q, turned):
             nb = pieces[q][2]
-            products = work.tile([P, 2, nb, 2, 2, P], F32, name="products")
-            for t in range(2):
-                nc.vector.tensor_tensor(
-                    out=products[:, t],
-                    in0=turned[:].bitcast(BF16).rearrange("w (b k) (p e) -> w b k e p", k=2, e=2),
-                    in1=tables[:, t].unsqueeze(1).to_broadcast([P, nb, 2, 2, P]),
-                    op=ALU.mult,
-                )
+            products = work.tile([P, 2, nb, PACK * P], F32, name="products")
+            nc.vector.tensor_tensor(
+                out=products[:],
+                in0=turned[:].rearrange("d (b f) -> d b f", b=nb).unsqueeze(1).to_broadcast([P, 2, nb, PACK * P]),
+                in1=tables[:].unsqueeze(2).to_broadcast([P, 2, nb, PACK * P]),
+                op=ALU.mult,
+            )
             return products
 
         def add_back(products, b):
-            summed = psum.tile([P, 2, PACK * PAIRS], F32, name="summed")
-            for e in range(2):
-                for jj in range(2):
-                    for t in range(2):
-                        nc.tensor.matmul(
-                            out=summed[:, e, jj * P : (jj + 1) * P],
-                            lhsT=products[:, t, b, jj, e if t == 0 else 1 - e, :],
-                            rhs=ident_f[:],
-                            start=(t == 0),
-                            stop=(t == 1),
-                            is_transpose=True,
-                        )
+            summed = psum.tile([P, PACK, D], F32, name="summed")
+            for j in range(PACK):
+                for t, order in enumerate((ident_f, swap_f)):
+                    nc.tensor.matmul(
+                        out=summed[:, j, :],
+                        lhsT=products[:, t, b, j * P : (j + 1) * P],
+                        rhs=order[:],
+                        start=(t == 0),
+                        stop=(t == 1),
+                        is_transpose=True,
+                    )
             return summed
 
         def quantise_piece(q, dy_grouped):
@@ -218,13 +216,19 @@ def tile_lineartransformerblock_pa_v_kernel(tc, x, cos, sin, Wq, bq, r, grad_out
         ident_f = keep.tile([P, P], F32, name="ident_f")
         make_identity(nc, ident_f[:])
 
-        tables = keep.tile([P, 2, 2, 2, P], BF16, name="tables")
+        ident_bf = keep.tile([P, P], BF16, name="ident_bf")
+        nc.vector.tensor_copy(out=ident_bf[:], in_=ident_f[:])
+        swap_f = keep.tile([P, P], F32, name="swap_f")
+        pairs_out = swap_f[:].rearrange("p (i e) -> p i e", e=2)
+        pairs_in = ident_f[:].rearrange("p (i e) -> p i e", e=2)
+        for e in range(2):
+            nc.vector.tensor_copy(out=pairs_out[:, :, e], in_=pairs_in[:, :, 1 - e])
+
+        tables = keep.tile([P, 2, PACK * P], BF16, name="tables")
         sin_even = table_rows[:, 1].rearrange("p (q e) -> p q e", e=2)[:, :, 0]
         nc.vector.tensor_scalar(out=sin_even, in0=sin_even, scalar1=-1.0, scalar2=None, op0=ALU.mult)
-        turned_tables = turn(table_rows[:].rearrange("p t f -> p (t f)").bitcast(F32))
-        table_source = turned_tables[:].bitcast(BF16).rearrange("w (t k) (p e) -> w t k e p", t=2, e=2)
-        for t in range(2):
-            nc.scalar.copy(out=tables[:, t], in_=table_source[:, t])
+        turned_tables = turn(table_rows[:].rearrange("p t f -> p (t f)"))
+        nc.scalar.copy(out=tables[:], in_=turned_tables[:].rearrange("d (t f) -> d t f", t=2))
 
         waiting = []
         finished = []
@@ -247,8 +251,7 @@ def tile_lineartransformerblock_pa_v_kernel(tc, x, cos, sin, Wq, bq, r, grad_out
                 for b in range(pieces[q][2]):
                     summed = add_back(products_of[q], b)
                     nc.scalar.copy(
-                        out=grouped_of[q][:, b].rearrange("p (i e) j -> p i e j", e=2),
-                        in_=summed[:].rearrange("p e (j i) -> p i e j", j=PACK),
+                        out=grouped_of[q][:, b], in_=summed[:].rearrange("p j d -> p d j")
                     )
             if 0 <= step - 2 < n_pieces:
                 quantise_piece(step - 2, grouped_of[step - 2])
@@ -269,4 +272,4 @@ def tile_lineartransformerblock_pa_v_kernel(tc, x, cos, sin, Wq, bq, r, grad_out
                 waiting.remove((h, n))
                 finished.append((h, n, multiply(h, n)))
             if 0 <= step + 1 < n_pieces:
-                turned_of[step + 1] = turn(dr_of[step + 1][:].bitcast(F32))
+                turned_of[step + 1] = turn(dr_of[step + 1][:])

@@ -15,18 +15,18 @@ ACT = mybir.ActivationFunctionType
 B, S, C, H, D = 4, 512, 1024, 8, 128
 P = 128
 PACK = 4
+PAIRS = D // 2
 N_TILE = 512
 N_BANKS = C // N_TILE
 NB = 2
+ROWS = 2 * NB
 RUN = 4
-V_MASKS = 99
-X_AHEAD = 0
-X_RATE = 1
+HEADS_TURNED = 4
+MASK_LEAD = 2
 MX_LAG = 3
-MX_EXTRA = 3
+MX_LIMIT = 2
 V_PRODUCTS = 3
-SPLIT_FIRST = 1
-SPLIT_LAST = 1
+V_MASKS_A = 1
 
 FLOPS = 2 * B * S * H * D * C
 BYTES = 2 * (B * S * C + B * H * S * D + 2 * S * D) + 4 * (B * H * S * D + H * D * C)
@@ -36,19 +36,22 @@ def tile_lineartransformerblock_pa_v_kernel(tc, x, cos, sin, Wq, bq, r, grad_out
     nc = tc.nc
     with ExitStack() as stack:
         keep = stack.enter_context(tc.tile_pool(name="keep", bufs=1))
-        loads = stack.enter_context(tc.tile_pool(name="loads", bufs=6))
-        work = stack.enter_context(tc.tile_pool(name="work", bufs=3))
-        psum = stack.enter_context(tc.psum_pool(name="psum", bufs=3))
+        loads = stack.enter_context(tc.tile_pool(name="loads", bufs=4))
+        work = stack.enter_context(tc.tile_pool(name="work", bufs=2))
+        psum = stack.enter_context(tc.psum_pool(name="psum", bufs=2))
         stack.enter_context(tc.manual_schedule())
 
         pieces = []
-        for h in range(H):
+        for h in range(HEADS_TURNED):
             for first in range(0, B, NB):
-                if (h == 0 and first == 0 and SPLIT_FIRST) or (h == H - 1 and first == B - NB and SPLIT_LAST):
+                if h == 0 and first == 0:
                     pieces += [(h, first + k, 1) for k in range(NB)]
                 else:
                     pieces.append((h, first, NB))
         n_pieces = len(pieces)
+
+        straight = [(g, first) for g in range(HEADS_TURNED // 2, H // 2) for first in range(0, B, NB)]
+        n_straight = len(straight)
 
         def load_piece(q):
             h, first, nb = pieces[q]
@@ -61,9 +64,21 @@ def tile_lineartransformerblock_pa_v_kernel(tc, x, cos, sin, Wq, bq, r, grad_out
                 )
             return r_rows, g_rows
 
+        def load_straight(a):
+            g, first = straight[a]
+            r_rows = loads.tile([P, NB, 2, PACK * D], F32, name="r_straight", bufs=3)
+            g_rows = loads.tile([P, NB, 2, PACK * D], BF16, name="g_straight", bufs=3)
+            for rows, source in ((r_rows, r), (g_rows, grad_out)):
+                for k in range(2):
+                    nc.sync.dma_start(
+                        out=rows[:, :, k, :],
+                        in_=source[first : first + NB, 2 * g + k].rearrange("b (p j) d -> p b (j d)", j=PACK),
+                    )
+            return r_rows, g_rows
+
         def load_x(chunk):
             n, b = divmod(chunk, B)
-            x_rows = loads.tile([P, PACK, N_TILE], BF16, name="x_rows", bufs=4)
+            x_rows = loads.tile([P, PACK, N_TILE], BF16, name="x_rows", bufs=3)
             nc.sync.dma_start(
                 out=x_rows[:],
                 in_=x[b].rearrange("(p j) c -> p j c", j=PACK)[:, :, n * N_TILE : (n + 1) * N_TILE],
@@ -71,20 +86,14 @@ def tile_lineartransformerblock_pa_v_kernel(tc, x, cos, sin, Wq, bq, r, grad_out
             return x_rows
 
         def relu_mask(q):
-            r_rows = loaded[q][0]
             n_cols = pieces[q][2] * PACK * D
-            mask = work.tile([P, n_cols], BF16, name="mask")
-            flat = r_rows[:].rearrange("p b f -> p (b f)")
-            if q < V_MASKS:
-                nc.vector.tensor_scalar(out=mask[:], in0=flat, scalar1=0.0, scalar2=None, op0=ALU.is_gt)
-            else:
-                r_sign = work.tile([P, n_cols], BF16, name="r_sign")
-                nc.scalar.activation(out=r_sign[:], in_=flat, func=ACT.Sign)
-                nc.scalar.activation(out=mask[:], in_=r_sign[:], func=ACT.Relu)
+            mask = work.tile([P, n_cols], BF16, name="mask", bufs=3)
+            flat = loaded[q][0][:].rearrange("p b f -> p (b f)")
+            nc.vector.tensor_scalar(out=mask[:], in0=flat, scalar1=0.0, scalar2=None, op0=ALU.is_gt)
             return mask
 
         def relu_backward(q):
-            dr = work.tile([P, pieces[q][2] * PACK * D], BF16, name="dr")
+            dr = work.tile([P, pieces[q][2] * PACK * D], BF16, name="dr", bufs=3)
             engine = nc.vector if q < V_PRODUCTS else nc.gpsimd
             engine.tensor_tensor(
                 out=dr[:],
@@ -104,7 +113,7 @@ def tile_lineartransformerblock_pa_v_kernel(tc, x, cos, sin, Wq, bq, r, grad_out
 
         def rope_products(q, turned):
             nb = pieces[q][2]
-            products = work.tile([P, 2, nb, PACK * P], F32, name="products")
+            products = work.tile([P, 2, nb, PACK * P], F32, name="products", bufs=2)
             nc.vector.tensor_tensor(
                 out=products[:],
                 in0=turned[:].rearrange("d (b f) -> d b f", b=nb).unsqueeze(1).to_broadcast([P, 2, nb, PACK * P]),
@@ -114,7 +123,7 @@ def tile_lineartransformerblock_pa_v_kernel(tc, x, cos, sin, Wq, bq, r, grad_out
             return products
 
         def add_back(products, b):
-            summed = psum.tile([P, PACK, D], F32, name="summed")
+            summed = psum.tile([P, PACK, D], F32, name="summed", bufs=3)
             for j in range(PACK):
                 for t, order in enumerate((ident_f, swap_f)):
                     nc.tensor.matmul(
@@ -140,11 +149,72 @@ def tile_lineartransformerblock_pa_v_kernel(tc, x, cos, sin, Wq, bq, r, grad_out
                 cols = slice(k * D, (k + 1) * D)
                 codes_of[(pieces[q][0], pieces[q][1] + k)] = (dy_codes[:, cols], dy_scales[:, cols])
 
+        def straight_mask(a):
+            r_flat = loaded_straight[a][0][:].rearrange("p b k f -> p (b k f)")
+            mask = work.tile([P, ROWS, PACK, D], BF16, name="mask_straight", bufs=2)
+            flat = mask[:].rearrange("p q j d -> p (q j d)")
+            if a < V_MASKS_A:
+                nc.vector.tensor_scalar(out=flat, in0=r_flat, scalar1=0.0, scalar2=None, op0=ALU.is_gt)
+            else:
+                for part in range(2):
+                    cols = slice(part * NB * PACK * D, (part + 1) * NB * PACK * D)
+                    r_sign = work.tile([P, NB * PACK * D], BF16, name="r_sign")
+                    nc.scalar.activation(out=r_sign[:], in_=r_flat[:, cols], func=ACT.Sign)
+                    nc.scalar.activation(out=flat[:, cols], in_=r_sign[:], func=ACT.Relu)
+            return mask
+
+        def straight_backward(a):
+            dr = work.tile([P, PACK, ROWS, PAIRS, 2], BF16, name="dr_straight")
+            nc.vector.tensor_tensor(
+                out=dr[:].rearrange("p j q i e -> p q j (i e)"),
+                in0=mask_straight[a][:],
+                in1=loaded_straight[a][1][:].rearrange("p b k (j d) -> p (b k) j d", j=PACK),
+                op=ALU.mult,
+            )
+            return dr
+
+        def straight_products(dr):
+            products = []
+            shape = [P, 2, PACK, ROWS, PAIRS]
+            for channel in range(2):
+                both = work.tile(shape, F32, name="both", bufs=4)
+                nc.vector.tensor_tensor(
+                    out=both[:],
+                    in0=dr[:, :, :, :, channel].unsqueeze(1).to_broadcast(shape),
+                    in1=table_planes[:, channel].unsqueeze(3).to_broadcast(shape),
+                    op=ALU.mult,
+                )
+                products.append(both)
+            return products
+
+        def combine(engine, parity, products):
+            dy_plane = work.tile([P, ROWS * PAIRS, PACK], BF16, align_bytes=64, name="dy_plane_%d" % parity)
+            engine.tensor_tensor(
+                out=dy_plane[:].rearrange("p (c i) j -> p c j i", i=RUN),
+                in0=products[parity][:, 0].rearrange("p j q (c i) -> p (q c) j i", i=RUN),
+                in1=products[1 - parity][:, 1].rearrange("p j q (c i) -> p (q c) j i", i=RUN),
+                op=(ALU.add if parity == 0 else ALU.subtract),
+            )
+            return dy_plane
+
+        def quantise_plane(a, parity, dy_plane):
+            plane_codes = keep.tile([P, NB * P], U32, align_bytes=64, name="plane_codes_%d_%d" % (a, parity))
+            plane_scales = keep.tile([P, NB * P], U8, align_bytes=64, name="plane_scales_%d_%d" % (a, parity))
+            nc.vector.quantize_mx(
+                out=plane_codes[:].bitcast(E5M2_X4),
+                scales=plane_scales[:],
+                in_=dy_plane[:].rearrange("p c j -> p (c j)"),
+            )
+            g, first = straight[a]
+            for k in range(NB):
+                cols = slice(k * P, (k + 1) * P)
+                plane_codes_of[(g, parity, first + k)] = (plane_codes[:, cols], plane_scales[:, cols])
+
         x_codes = keep.tile([P, B, C], U32, align_bytes=64)
         x_scales = keep.tile([P, B, C], U8, align_bytes=64)
 
         def regroup_x(chunk):
-            x_grouped = work.tile([P, N_TILE, PACK], BF16, align_bytes=64, name="x_grouped")
+            x_grouped = work.tile([P, N_TILE, PACK], BF16, align_bytes=64, name="x_grouped", bufs=3)
             nc.scalar.copy(
                 out=x_grouped[:].rearrange("p (c i) j -> p c j i", i=RUN),
                 in_=x_rows[chunk][:].rearrange("p j (c i) -> p c j i", i=RUN),
@@ -160,10 +230,9 @@ def tile_lineartransformerblock_pa_v_kernel(tc, x, cos, sin, Wq, bq, r, grad_out
                 in_=x_grouped_of[chunk][:].rearrange("p c j -> p (c j)"),
             )
 
-        def multiply(h, n):
-            acc = psum.tile([P, N_TILE], F32, name="acc", bufs=2)
-            for b in range(B):
-                dy_codes, dy_scales = codes_of[(h, b)]
+        def multiply(codes_for, n, acc, batches):
+            for b in batches:
+                dy_codes, dy_scales = codes_for(b)
                 nc.tensor.matmul_mx(
                     out=acc[:],
                     lhsT=dy_codes.bitcast(E5M2_X4),
@@ -173,14 +242,13 @@ def tile_lineartransformerblock_pa_v_kernel(tc, x, cos, sin, Wq, bq, r, grad_out
                     start=(b == 0),
                     stop=(b == B - 1),
                 )
-            return acc
 
-        def store(h, n, acc):
+        out_pairs = out.rearrange("(g m e) c -> g e m c", m=P, e=2)
+
+        def store(rows_out, n, acc, engine_copy):
             out_rows = work.tile([P, N_TILE], F32, name="out_rows", bufs=4)
-            nc.scalar.copy(out=out_rows[:], in_=acc[:])
-            nc.scalar.dma_start(
-                out=out[h * D : (h + 1) * D, n * N_TILE : (n + 1) * N_TILE], in_=out_rows[:]
-            )
+            engine_copy(out=out_rows[:], in_=acc[:])
+            nc.scalar.dma_start(out=rows_out[:, n * N_TILE : (n + 1) * N_TILE], in_=out_rows[:])
 
         loaded = {}
         mask_of = {}
@@ -189,6 +257,11 @@ def tile_lineartransformerblock_pa_v_kernel(tc, x, cos, sin, Wq, bq, r, grad_out
         products_of = {}
         grouped_of = {}
         codes_of = {}
+        loaded_straight = {}
+        mask_straight = {}
+        both_of = {}
+        even_plane = {}
+        plane_codes_of = {}
         x_rows = {}
         x_grouped_of = {}
 
@@ -198,24 +271,25 @@ def tile_lineartransformerblock_pa_v_kernel(tc, x, cos, sin, Wq, bq, r, grad_out
                 load_order.append(("x", k))
             if k + 2 < n_pieces:
                 load_order.append(("r", k + 2))
-
-        table_rows = keep.tile([P, 2, PACK * D], BF16, name="table_rows")
-        for t, source in enumerate((cos, sin)):
-            nc.sync.dma_start(out=table_rows[:, t], in_=source.rearrange("(p j) d -> p (j d)", j=PACK))
+        load_order += [("s", a) for a in range(n_straight)]
 
         def issue(count):
             for kind, k in load_order[:count]:
                 if kind == "r":
                     loaded[k] = load_piece(k)
+                elif kind == "s":
+                    loaded_straight[k] = load_straight(k)
                 else:
                     x_rows[k] = load_x(k)
             return load_order[count:]
 
+        table_rows = keep.tile([P, 2, PACK * D], BF16, name="table_rows")
+        for t, source in enumerate((cos, sin)):
+            nc.sync.dma_start(out=table_rows[:, t], in_=source.rearrange("(p j) d -> p (j d)", j=PACK))
         load_order = issue(5)
 
         ident_f = keep.tile([P, P], F32, name="ident_f")
         make_identity(nc, ident_f[:])
-
         ident_bf = keep.tile([P, P], BF16, name="ident_bf")
         nc.vector.tensor_copy(out=ident_bf[:], in_=ident_f[:])
         swap_f = keep.tile([P, P], F32, name="swap_f")
@@ -225,51 +299,112 @@ def tile_lineartransformerblock_pa_v_kernel(tc, x, cos, sin, Wq, bq, r, grad_out
             nc.vector.tensor_copy(out=pairs_out[:, :, e], in_=pairs_in[:, :, 1 - e])
 
         tables = keep.tile([P, 2, PACK * P], BF16, name="tables")
-        sin_even = table_rows[:, 1].rearrange("p (q e) -> p q e", e=2)[:, :, 0]
-        nc.vector.tensor_scalar(out=sin_even, in0=sin_even, scalar1=-1.0, scalar2=None, op0=ALU.mult)
-        turned_tables = turn(table_rows[:].rearrange("p t f -> p (t f)"))
-        nc.scalar.copy(out=tables[:], in_=turned_tables[:].rearrange("d (t f) -> d t f", t=2))
+        signed_rows = keep.tile([P, PACK * D], BF16, name="signed_rows")
+        signed_pairs = signed_rows[:].rearrange("p (q e) -> p q e", e=2)
+        sin_pairs = table_rows[:, 1].rearrange("p (q e) -> p q e", e=2)
+        nc.vector.tensor_scalar(
+            out=signed_pairs[:, :, 0], in0=sin_pairs[:, :, 0], scalar1=-1.0, scalar2=None, op0=ALU.mult
+        )
+        nc.vector.tensor_copy(out=signed_pairs[:, :, 1], in_=sin_pairs[:, :, 1])
+        for t, rows in enumerate((table_rows[:, 0], signed_rows[:])):
+            turned_tables = turn(rows)
+            nc.scalar.copy(out=tables[:, t], in_=turned_tables[:])
+        table_planes = psum.tile([P, 2, 2, PACK, PAIRS], BF16, name="table_planes", bufs=1)
+
+        def make_planes():
+            for channel in range(2):
+                for t in range(2):
+                    nc.tensor.matmul(
+                        out=table_planes[:, channel, t].rearrange("p j i -> p (j i)"),
+                        lhsT=ident_bf[:],
+                        rhs=table_rows[:, t].rearrange("p (q e) -> p q e", e=2)[:, :, channel],
+                        start=True,
+                        stop=True,
+                    )
 
         waiting = []
+        coming = []
         finished = []
-        x_done = 0
-        for step in range(-2, n_pieces + 9):
-            load_order = issue(2)
-            for h, n, acc in finished:
-                store(h, n, acc)
+        last_acc = {}
+        for step in range(-2, n_pieces + n_straight + 6):
+            load_order = issue(3)
+            a = step - n_pieces
+            for rows_out, n, acc in finished:
+                store(rows_out, n, acc, nc.scalar.copy)
             finished = []
-            if V_MASKS <= step + 3 < n_pieces:
-                mask_of[step + 3] = relu_mask(step + 3)
-            for chunk in range(X_RATE * step + X_AHEAD, X_RATE * (step + 1) + X_AHEAD):
-                if 0 <= chunk < B * N_BANKS:
-                    x_grouped_of[chunk] = regroup_x(chunk)
+            if 0 <= step < B * N_BANKS:
+                x_grouped_of[step] = regroup_x(step)
             if 0 <= step < n_pieces:
                 products_of[step] = rope_products(step, turned_of[step])
+            if 0 <= a < n_straight:
+                dr_straight = straight_backward(a)
             if 0 <= step - 1 < n_pieces:
                 q = step - 1
-                grouped_of[q] = work.tile([P, pieces[q][2], D, PACK], BF16, align_bytes=64, name="dy_grouped")
+                grouped_of[q] = work.tile([P, pieces[q][2], D, PACK], BF16, align_bytes=64, name="dy_grouped", bufs=3)
                 for b in range(pieces[q][2]):
                     summed = add_back(products_of[q], b)
-                    nc.scalar.copy(
-                        out=grouped_of[q][:, b], in_=summed[:].rearrange("p j d -> p d j")
-                    )
+                    nc.scalar.copy(out=grouped_of[q][:, b], in_=summed[:].rearrange("p j d -> p d j"))
             if 0 <= step - 2 < n_pieces:
                 quantise_piece(step - 2, grouped_of[step - 2])
-            for chunk in range(X_RATE * (step - 1) + X_AHEAD, X_RATE * step + X_AHEAD):
-                if 0 <= chunk < B * N_BANKS:
-                    quantise_x(chunk)
-                    x_done = chunk + 1
+            if 0 <= step - 1 < B * N_BANKS:
+                quantise_x(step - 1)
+            x_done = step
+            if 1 <= a <= n_straight:
+                quantise_plane(a - 1, 0, even_plane[a - 1])
+                odd_plane = combine(nc.gpsimd if a < n_straight else nc.vector, 1, both_of[a - 1])
+            if 0 <= a < n_straight:
+                both_of[a] = straight_products(dr_straight)
+            if 1 <= a <= n_straight:
+                quantise_plane(a - 1, 1, odd_plane)
+            if 0 <= a < n_straight:
+                even_plane[a] = combine(nc.vector, 0, both_of[a])
             if 0 <= step + 2 < n_pieces:
-                if step + 2 < V_MASKS:
-                    mask_of[step + 2] = relu_mask(step + 2)
+                mask_of[step + 2] = relu_mask(step + 2)
                 dr_of[step + 2] = relu_backward(step + 2)
-            q = step - MX_LAG
+            if 0 <= a + 1 < min(n_straight, V_MASKS_A):
+                mask_straight[a + 1] = straight_mask(a + 1)
+            if V_MASKS_A <= a + MASK_LEAD < n_straight:
+                mask_straight[a + MASK_LEAD] = straight_mask(a + MASK_LEAD)
+            waiting += coming
+            coming = []
+            q = step - MX_LAG + 1
             if 0 <= q < n_pieces and pieces[q][1] + pieces[q][2] == B:
-                waiting += [(pieces[q][0], n) for n in range(N_BANKS)]
-            limit = 2 if step % MX_EXTRA == 0 or step > n_pieces else 1
-            ready = [(h, n) for h, n in waiting if x_done >= (n + 1) * B][:limit]
-            for h, n in ready:
-                waiting.remove((h, n))
-                finished.append((h, n, multiply(h, n)))
+                h = pieces[q][0]
+                for n in range(N_BANKS):
+                    coming.append((n, out[h * D : (h + 1) * D], lambda b, h=h: codes_of[(h, b)]))
+            limit = MX_LIMIT if step < n_pieces else 4
+            ready = [item for item in waiting if x_done >= (item[0] + 1) * B][:limit]
+            for item in ready:
+                waiting.remove(item)
+                acc = psum.tile([P, N_TILE], F32, name="acc")
+                multiply(item[2], item[0], acc, range(B))
+                finished.append((item[1], item[0], acc))
+            if 1 <= a <= n_straight:
+                g, first = straight[a - 1]
+                if g < H // 2 - 1:
+                    if first + NB == B:
+                        for parity in range(2):
+                            for n in range(N_BANKS):
+                                coming.append(
+                                    (n, out_pairs[g, parity], lambda b, g=g, e=parity: plane_codes_of[(g, e, b)])
+                                )
+                else:
+                    for parity in range(2):
+                        for n in range(N_BANKS):
+                            if first == 0:
+                                last_acc[(parity, n)] = psum.tile(
+                                    [P, N_TILE], F32, name=("turned" if parity == 0 else "summed"),
+                                    bufs=(2 if parity == 0 else 3),
+                                )
+                            multiply(
+                                lambda b, g=g, e=parity: plane_codes_of[(g, e, b)],
+                                n,
+                                last_acc[(parity, n)],
+                                range(first, first + NB),
+                            )
+                            if first + NB == B:
+                                finished.append((out_pairs[g, parity], n, last_acc[(parity, n)]))
             if 0 <= step + 1 < n_pieces:
                 turned_of[step + 1] = turn(dr_of[step + 1][:])
+            if step == 1:
+                make_planes()

@@ -27,6 +27,12 @@ MX_LAG = 3
 MX_LIMIT = 2
 V_PRODUCTS = 3
 V_MASKS_A = 1
+EARLY = 2
+PE_ROWS = 2
+PE_PIECES = (1, 2)
+X_LAG = 1
+X_FIRST = 8
+X_PAUSE = 0
 
 FLOPS = 2 * B * S * H * D * C
 BYTES = 2 * (B * S * C + B * H * S * D + 2 * S * D) + 4 * (B * H * S * D + H * D * C)
@@ -197,6 +203,32 @@ def tile_lineartransformerblock_pa_v_kernel(tc, x, cos, sin, Wq, bq, r, grad_out
             )
             return dy_plane
 
+        def rest_on_vector(dy_plane, products):
+            nc.vector.tensor_tensor(
+                out=dy_plane[:, PE_ROWS * PAIRS :].rearrange("p (c i) j -> p c j i", i=RUN),
+                in0=products[0][:, 0, :, PE_ROWS:].rearrange("p j q (c i) -> p (q c) j i", i=RUN),
+                in1=products[1][:, 1, :, PE_ROWS:].rearrange("p j q (c i) -> p (q c) j i", i=RUN),
+                op=ALU.add,
+            )
+
+        def sum_on_tensor(products):
+            dy_plane = work.tile([P, ROWS * PAIRS, PACK], BF16, align_bytes=64, name="dy_plane_0")
+            for row in range(0, PE_ROWS, 2):
+                plane_sum = psum.tile([P, PACK, 2, PAIRS], F32, name="summed", bufs=3)
+                for t in range(2):
+                    nc.tensor.matmul(
+                        out=plane_sum[:].rearrange("p j q i -> p j (q i)"),
+                        lhsT=ident_f[:],
+                        rhs=products[t][:, t, :, row : row + 2].rearrange("p j q i -> p j (q i)"),
+                        start=(t == 0),
+                        stop=(t == 1),
+                    )
+                nc.scalar.copy(
+                    out=dy_plane[:, row * PAIRS : (row + 2) * PAIRS],
+                    in_=plane_sum[:].rearrange("p j q i -> p (q i) j"),
+                )
+            return dy_plane
+
         def quantise_plane(a, parity, dy_plane):
             plane_codes = keep.tile([P, NB * P], U32, align_bytes=64, name="plane_codes_%d_%d" % (a, parity))
             plane_scales = keep.tile([P, NB * P], U8, align_bytes=64, name="plane_scales_%d_%d" % (a, parity))
@@ -265,12 +297,12 @@ def tile_lineartransformerblock_pa_v_kernel(tc, x, cos, sin, Wq, bq, r, grad_out
         x_rows = {}
         x_grouped_of = {}
 
-        load_order = [("r", 0), ("r", 1)]
-        for k in range(max(n_pieces - 2, B * N_BANKS)):
+        load_order = [("r", k) for k in range(EARLY)]
+        for k in range(max(n_pieces - EARLY, B * N_BANKS)):
             if k < B * N_BANKS:
                 load_order.append(("x", k))
-            if k + 2 < n_pieces:
-                load_order.append(("r", k + 2))
+            if k + EARLY < n_pieces:
+                load_order.append(("r", k + EARLY))
         load_order += [("s", a) for a in range(n_straight)]
 
         def issue(count):
@@ -286,12 +318,12 @@ def tile_lineartransformerblock_pa_v_kernel(tc, x, cos, sin, Wq, bq, r, grad_out
         table_rows = keep.tile([P, 2, PACK * D], BF16, name="table_rows")
         for t, source in enumerate((cos, sin)):
             nc.sync.dma_start(out=table_rows[:, t], in_=source.rearrange("(p j) d -> p (j d)", j=PACK))
-        load_order = issue(5)
+        load_order = issue(6)
 
         ident_f = keep.tile([P, P], F32, name="ident_f")
         make_identity(nc, ident_f[:])
         ident_bf = keep.tile([P, P], BF16, name="ident_bf")
-        nc.vector.tensor_copy(out=ident_bf[:], in_=ident_f[:])
+        nc.scalar.copy(out=ident_bf[:], in_=ident_f[:])
         swap_f = keep.tile([P, P], F32, name="swap_f")
         pairs_out = swap_f[:].rearrange("p (i e) -> p i e", e=2)
         pairs_in = ident_f[:].rearrange("p (i e) -> p i e", e=2)
@@ -299,16 +331,17 @@ def tile_lineartransformerblock_pa_v_kernel(tc, x, cos, sin, Wq, bq, r, grad_out
             nc.vector.tensor_copy(out=pairs_out[:, :, e], in_=pairs_in[:, :, 1 - e])
 
         tables = keep.tile([P, 2, PACK * P], BF16, name="tables")
-        signed_rows = keep.tile([P, PACK * D], BF16, name="signed_rows")
-        signed_pairs = signed_rows[:].rearrange("p (q e) -> p q e", e=2)
-        sin_pairs = table_rows[:, 1].rearrange("p (q e) -> p q e", e=2)
+        even_rows = keep.tile([P, 1], F32, name="even_rows")
+        nc.vector.tensor_reduce(out=even_rows[:], in_=pairs_in[:, :, 0], op=ALU.add, axis=mybir.AxisListType.X)
+        sign = keep.tile([P, 1], F32, name="sign")
         nc.vector.tensor_scalar(
-            out=signed_pairs[:, :, 0], in0=sin_pairs[:, :, 0], scalar1=-1.0, scalar2=None, op0=ALU.mult
+            out=sign[:], in0=even_rows[:], scalar1=-2.0, scalar2=1.0, op0=ALU.mult, op1=ALU.add
         )
-        nc.vector.tensor_copy(out=signed_pairs[:, :, 1], in_=sin_pairs[:, :, 1])
-        for t, rows in enumerate((table_rows[:, 0], signed_rows[:])):
-            turned_tables = turn(rows)
-            nc.scalar.copy(out=tables[:, t], in_=turned_tables[:])
+        turned_tables = turn(table_rows[:].rearrange("p t f -> p (t f)"))
+        nc.scalar.copy(out=tables[:, 0], in_=turned_tables[:, : PACK * P])
+        nc.scalar.activation(
+            out=tables[:, 1], in_=turned_tables[:, PACK * P :], func=ACT.Copy, scale=sign[:]
+        )
         table_planes = psum.tile([P, 2, 2, PACK, PAIRS], BF16, name="table_planes", bufs=1)
 
         def make_planes():
@@ -326,18 +359,27 @@ def tile_lineartransformerblock_pa_v_kernel(tc, x, cos, sin, Wq, bq, r, grad_out
         coming = []
         finished = []
         last_acc = {}
+        x_done = 0
+        x_step = {}
+        for chunk in range(B * N_BANKS):
+            x_step[chunk if chunk < X_FIRST else chunk + X_PAUSE] = chunk
         for step in range(-2, n_pieces + n_straight + 6):
             load_order = issue(3)
             a = step - n_pieces
-            for rows_out, n, acc in finished:
-                store(rows_out, n, acc, nc.scalar.copy)
+            for k, (rows_out, n, acc) in enumerate(finished):
+                on_vector = a > n_straight and k % 2 == 1
+                store(rows_out, n, acc, nc.vector.tensor_copy if on_vector else nc.scalar.copy)
             finished = []
-            if 0 <= step < B * N_BANKS:
-                x_grouped_of[step] = regroup_x(step)
+            if step in x_step:
+                x_grouped_of[x_step[step]] = regroup_x(x_step[step])
+            if a - 1 in PE_PIECES:
+                even_plane[a - 1] = sum_on_tensor(both_of[a - 1])
             if 0 <= step < n_pieces:
                 products_of[step] = rope_products(step, turned_of[step])
             if 0 <= a < n_straight:
                 dr_straight = straight_backward(a)
+            if a - 1 in PE_PIECES:
+                rest_on_vector(even_plane[a - 1], both_of[a - 1])
             if 0 <= step - 1 < n_pieces:
                 q = step - 1
                 grouped_of[q] = work.tile([P, pieces[q][2], D, PACK], BF16, align_bytes=64, name="dy_grouped", bufs=3)
@@ -346,18 +388,22 @@ def tile_lineartransformerblock_pa_v_kernel(tc, x, cos, sin, Wq, bq, r, grad_out
                     nc.scalar.copy(out=grouped_of[q][:, b], in_=summed[:].rearrange("p j d -> p d j"))
             if 0 <= step - 2 < n_pieces:
                 quantise_piece(step - 2, grouped_of[step - 2])
-            if 0 <= step - 1 < B * N_BANKS:
-                quantise_x(step - 1)
-            x_done = step
+            if step - X_LAG in x_step:
+                quantise_x(x_step[step - X_LAG])
+                x_done = x_step[step - X_LAG] + 1
             if 1 <= a <= n_straight:
-                quantise_plane(a - 1, 0, even_plane[a - 1])
+                if a - 1 not in PE_PIECES:
+                    quantise_plane(a - 1, 0, even_plane[a - 1])
                 odd_plane = combine(nc.gpsimd if a < n_straight else nc.vector, 1, both_of[a - 1])
             if 0 <= a < n_straight:
                 both_of[a] = straight_products(dr_straight)
             if 1 <= a <= n_straight:
+                if a - 1 in PE_PIECES:
+                    quantise_plane(a - 1, 0, even_plane[a - 1])
                 quantise_plane(a - 1, 1, odd_plane)
             if 0 <= a < n_straight:
-                even_plane[a] = combine(nc.vector, 0, both_of[a])
+                if a not in PE_PIECES:
+                    even_plane[a] = combine(nc.vector, 0, both_of[a])
             if 0 <= step + 2 < n_pieces:
                 mask_of[step + 2] = relu_mask(step + 2)
                 dr_of[step + 2] = relu_backward(step + 2)

@@ -26,10 +26,9 @@ MASK_LEAD = 2
 MX_LAG = 3
 MX_LIMIT = 2
 V_PRODUCTS = 3
-V_MASKS_A = 1
+V_MASKS_A = 2
 EARLY = 2
-PE_ROWS = 2
-PE_PIECES = (1, 2)
+PE_PIECES = (0, 1)
 X_LAG = 1
 X_FIRST = 8
 X_PAUSE = 0
@@ -193,6 +192,10 @@ def tile_lineartransformerblock_pa_v_kernel(tc, x, cos, sin, Wq, bq, r, grad_out
                 products.append(both)
             return products
 
+        def guard(products):
+            pair = products[1][:, 0, 0, 0, 0:2]
+            nc.vector.tensor_copy(out=pair, in_=pair)
+
         def combine(engine, parity, products):
             dy_plane = work.tile([P, ROWS * PAIRS, PACK], BF16, align_bytes=64, name="dy_plane_%d" % parity)
             engine.tensor_tensor(
@@ -203,17 +206,9 @@ def tile_lineartransformerblock_pa_v_kernel(tc, x, cos, sin, Wq, bq, r, grad_out
             )
             return dy_plane
 
-        def rest_on_vector(dy_plane, products):
-            nc.vector.tensor_tensor(
-                out=dy_plane[:, PE_ROWS * PAIRS :].rearrange("p (c i) j -> p c j i", i=RUN),
-                in0=products[0][:, 0, :, PE_ROWS:].rearrange("p j q (c i) -> p (q c) j i", i=RUN),
-                in1=products[1][:, 1, :, PE_ROWS:].rearrange("p j q (c i) -> p (q c) j i", i=RUN),
-                op=ALU.add,
-            )
-
         def sum_on_tensor(products):
             dy_plane = work.tile([P, ROWS * PAIRS, PACK], BF16, align_bytes=64, name="dy_plane_0")
-            for row in range(0, PE_ROWS, 2):
+            for row in range(0, ROWS, 2):
                 plane_sum = psum.tile([P, PACK, 2, PAIRS], F32, name="summed", bufs=3)
                 for t in range(2):
                     nc.tensor.matmul(
@@ -293,6 +288,7 @@ def tile_lineartransformerblock_pa_v_kernel(tc, x, cos, sin, Wq, bq, r, grad_out
         mask_straight = {}
         both_of = {}
         even_plane = {}
+        odd_plane = {}
         plane_codes_of = {}
         x_rows = {}
         x_grouped_of = {}
@@ -378,8 +374,6 @@ def tile_lineartransformerblock_pa_v_kernel(tc, x, cos, sin, Wq, bq, r, grad_out
                 products_of[step] = rope_products(step, turned_of[step])
             if 0 <= a < n_straight:
                 dr_straight = straight_backward(a)
-            if a - 1 in PE_PIECES:
-                rest_on_vector(even_plane[a - 1], both_of[a - 1])
             if 0 <= step - 1 < n_pieces:
                 q = step - 1
                 grouped_of[q] = work.tile([P, pieces[q][2], D, PACK], BF16, align_bytes=64, name="dy_grouped", bufs=3)
@@ -392,23 +386,28 @@ def tile_lineartransformerblock_pa_v_kernel(tc, x, cos, sin, Wq, bq, r, grad_out
                 quantise_x(x_step[step - X_LAG])
                 x_done = x_step[step - X_LAG] + 1
             if 1 <= a <= n_straight:
+                if a - 2 in PE_PIECES:
+                    quantise_plane(a - 2, 1, odd_plane[a - 2])
                 if a - 1 not in PE_PIECES:
                     quantise_plane(a - 1, 0, even_plane[a - 1])
-                odd_plane = combine(nc.gpsimd if a < n_straight else nc.vector, 1, both_of[a - 1])
+                if a < n_straight:
+                    guard(both_of[a - 1])
+                odd_plane[a - 1] = combine(nc.gpsimd if a < n_straight else nc.vector, 1, both_of[a - 1])
             if 0 <= a < n_straight:
                 both_of[a] = straight_products(dr_straight)
+            if 0 <= a + 1 < min(n_straight, V_MASKS_A):
+                mask_straight[a + 1] = straight_mask(a + 1)
             if 1 <= a <= n_straight:
                 if a - 1 in PE_PIECES:
                     quantise_plane(a - 1, 0, even_plane[a - 1])
-                quantise_plane(a - 1, 1, odd_plane)
+                else:
+                    quantise_plane(a - 1, 1, odd_plane[a - 1])
             if 0 <= a < n_straight:
                 if a not in PE_PIECES:
                     even_plane[a] = combine(nc.vector, 0, both_of[a])
             if 0 <= step + 2 < n_pieces:
                 mask_of[step + 2] = relu_mask(step + 2)
                 dr_of[step + 2] = relu_backward(step + 2)
-            if 0 <= a + 1 < min(n_straight, V_MASKS_A):
-                mask_straight[a + 1] = straight_mask(a + 1)
             if V_MASKS_A <= a + MASK_LEAD < n_straight:
                 mask_straight[a + MASK_LEAD] = straight_mask(a + MASK_LEAD)
             waiting += coming

@@ -25,6 +25,7 @@ HEADS_TURNED = 4
 MASK_LEAD = 2
 MX_LAG = 3
 MX_LIMIT = 2
+G_COLS = 768
 V_PRODUCTS = 3
 V_MASKS_A = 2
 EARLY = 2
@@ -98,15 +99,18 @@ def tile_lineartransformerblock_pa_v_kernel(tc, x, cos, sin, Wq, bq, r, grad_out
             return mask
 
         def relu_backward(q):
-            dr = work.tile([P, pieces[q][2] * PACK * D], BF16, name="dr", bufs=3)
-            engine = nc.vector if q < V_PRODUCTS else nc.gpsimd
+            n_cols = pieces[q][2] * PACK * D
+            dr = work.tile([P, n_cols], BF16, name="dr", bufs=3)
+            multiply_mask(nc.vector if q < V_PRODUCTS else nc.gpsimd, q, dr, slice(0, n_cols if q < V_PRODUCTS else G_COLS))
+            return dr
+
+        def multiply_mask(engine, q, dr, cols):
             engine.tensor_tensor(
-                out=dr[:],
-                in0=mask_of[q][:],
-                in1=loaded[q][1][:].rearrange("p b f -> p (b f)"),
+                out=dr[:, cols],
+                in0=mask_of[q][:, cols],
+                in1=loaded[q][1][:].rearrange("p b f -> p (b f)")[:, cols],
                 op=ALU.mult,
             )
-            return dr
 
         def turn(rows):
             n_blocks = rows.shape[1] // P
@@ -372,6 +376,8 @@ def tile_lineartransformerblock_pa_v_kernel(tc, x, cos, sin, Wq, bq, r, grad_out
                 even_plane[a - 1] = sum_on_tensor(both_of[a - 1])
             if 0 <= step < n_pieces:
                 products_of[step] = rope_products(step, turned_of[step])
+            if V_PRODUCTS <= step + 1 < n_pieces:
+                multiply_mask(nc.vector, step + 1, dr_of[step + 1], slice(G_COLS, NB * PACK * D))
             if 0 <= a < n_straight:
                 dr_straight = straight_backward(a)
             if 0 <= step - 1 < n_pieces:

from contextlib import ExitStack

import concourse.mybir as mybir
from concourse.masks import make_identity

F32 = mybir.dt.float32
BF16 = mybir.dt.bfloat16
U32 = mybir.dt.uint32
U8 = mybir.dt.uint8
E4M3_X4 = mybir.dt.float8_e4m3fn_x4
E5M2_X4 = mybir.dt.float8_e5m2_x4
ALU = mybir.AluOpType
ACT = mybir.ActivationFunctionType

B, S, C, H, D = 4, 512, 1024, 8, 128
P = 128
PACK = 4
PAIRS = D // 2
N_TILE = 512
N_BANKS = C // N_TILE
NB = 2
ROWS = 2 * NB
RUN = 4
HEADS_TURNED = 4
MASK_LEAD = 2
MX_LAG = 3
MX_LIMIT = 2
G_COLS = 768
V_PRODUCTS = 3
V_MASKS_A = 2
EARLY = 2
PE_PIECES = (0, 1)
X_LAG = 1
X_FIRST = 8
X_PAUSE = 0

FLOPS = 2 * B * S * H * D * C
BYTES = 2 * (B * S * C + B * H * S * D + 2 * S * D) + 4 * (B * H * S * D + H * D * C)


def tile_lineartransformerblock_pa_v_kernel(tc, x, cos, sin, Wq, bq, r, grad_out, out):
    nc = tc.nc
    with ExitStack() as stack:
        keep = stack.enter_context(tc.tile_pool(name="keep", bufs=1))
        loads = stack.enter_context(tc.tile_pool(name="loads", bufs=4))
        work = stack.enter_context(tc.tile_pool(name="work", bufs=2))
        psum = stack.enter_context(tc.psum_pool(name="psum", bufs=2))
        stack.enter_context(tc.manual_schedule())

        pieces = []
        for h in range(HEADS_TURNED):
            for first in range(0, B, NB):
                if h == 0 and first == 0:
                    pieces += [(h, first + k, 1) for k in range(NB)]
                else:
                    pieces.append((h, first, NB))
        n_pieces = len(pieces)

        straight = [(g, first) for g in range(HEADS_TURNED // 2, H // 2) for first in range(0, B, NB)]
        n_straight = len(straight)

        def load_piece(q):
            h, first, nb = pieces[q]
            r_rows = loads.tile([P, nb, PACK * D], F32, name="r_rows")
            g_rows = loads.tile([P, nb, PACK * D], BF16, name="g_rows")
            for rows, source in ((r_rows, r), (g_rows, grad_out)):
                nc.sync.dma_start(
                    out=rows[:],
                    in_=source[first : first + nb, h].rearrange("b (p j) d -> p b (j d)", j=PACK),
                )
            return r_rows, g_rows

        def load_straight(a):
            g, first = straight[a]
            r_rows = loads.tile([P, NB, 2, PACK * D], F32, name="r_straight", bufs=3)
            g_rows = loads.tile([P, NB, 2, PACK * D], BF16, name="g_straight", bufs=3)
            for rows, source in ((r_rows, r), (g_rows, grad_out)):
                for k in range(2):
                    nc.sync.dma_start(
                        out=rows[:, :, k, :],
                        in_=source[first : first + NB, 2 * g + k].rearrange("b (p j) d -> p b (j d)", j=PACK),
                    )
            return r_rows, g_rows

        def load_x(chunk):
            n, b = divmod(chunk, B)
            x_rows = loads.tile([P, PACK, N_TILE], BF16, name="x_rows", bufs=3)
            nc.sync.dma_start(
                out=x_rows[:],
                in_=x[b].rearrange("(p j) c -> p j c", j=PACK)[:, :, n * N_TILE : (n + 1) * N_TILE],
            )
            return x_rows

        def relu_mask(q):
            n_cols = pieces[q][2] * PACK * D
            mask = work.tile([P, n_cols], BF16, name="mask", bufs=3)
            flat = loaded[q][0][:].rearrange("p b f -> p (b f)")
            nc.vector.tensor_scalar(out=mask[:], in0=flat, scalar1=0.0, scalar2=None, op0=ALU.is_gt)
            return mask

        def relu_backward(q):
            n_cols = pieces[q][2] * PACK * D
            dr = work.tile([P, n_cols], BF16, name="dr", bufs=3)
            multiply_mask(nc.vector if q < V_PRODUCTS else nc.gpsimd, q, dr, slice(0, n_cols if q < V_PRODUCTS else G_COLS))
            return dr

        def multiply_mask(engine, q, dr, cols):
            engine.tensor_tensor(
                out=dr[:, cols],
                in0=mask_of[q][:, cols],
                in1=loaded[q][1][:].rearrange("p b f -> p (b f)")[:, cols],
                op=ALU.mult,
            )

        def turn(rows):
            n_blocks = rows.shape[1] // P
            turned = psum.tile([P, n_blocks * P], BF16, name="turned")
            for k in range(n_blocks):
                cols = slice(k * P, (k + 1) * P)
                nc.tensor.transpose(turned[:, cols], rows[:, cols], ident_bf[:])
            return turned

        def rope_products(q, turned):
            nb = pieces[q][2]
            products = work.tile([P, 2, nb, PACK * P], F32, name="products", bufs=2)
            nc.vector.tensor_tensor(
                out=products[:],
                in0=turned[:].rearrange("d (b f) -> d b f", b=nb).unsqueeze(1).to_broadcast([P, 2, nb, PACK * P]),
                in1=tables[:].unsqueeze(2).to_broadcast([P, 2, nb, PACK * P]),
                op=ALU.mult,
            )
            return products

        def add_back(products, b):
            summed = psum.tile([P, PACK, D], F32, name="summed", bufs=3)
            for j in range(PACK):
                for t, order in enumerate((ident_f, swap_f)):
                    nc.tensor.matmul(
                        out=summed[:, j, :],
                        lhsT=products[:, t, b, j * P : (j + 1) * P],
                        rhs=order[:],
                        start=(t == 0),
                        stop=(t == 1),
                        is_transpose=True,
                    )
            return summed

        def quantise_piece(q, dy_grouped):
            nb = pieces[q][2]
            dy_codes = keep.tile([P, nb * D], U32, align_bytes=64, name="dy_codes_%d" % q)
            dy_scales = keep.tile([P, nb * D], U8, align_bytes=64, name="dy_scales_%d" % q)
            nc.vector.quantize_mx(
                out=dy_codes[:].bitcast(E5M2_X4),
                scales=dy_scales[:],
                in_=dy_grouped[:].rearrange("p b d j -> p (b d j)"),
            )
            for k in range(nb):
                cols = slice(k * D, (k + 1) * D)
                codes_of[(pieces[q][0], pieces[q][1] + k)] = (dy_codes[:, cols], dy_scales[:, cols])

        def straight_mask(a):
            r_flat = loaded_straight[a][0][:].rearrange("p b k f -> p (b k f)")
            mask = work.tile([P, ROWS, PACK, D], BF16, name="mask_straight", bufs=2)
            flat = mask[:].rearrange("p q j d -> p (q j d)")
            if a < V_MASKS_A:
                nc.vector.tensor_scalar(out=flat, in0=r_flat, scalar1=0.0, scalar2=None, op0=ALU.is_gt)
            else:
                for part in range(2):
                    cols = slice(part * NB * PACK * D, (part + 1) * NB * PACK * D)
                    r_sign = work.tile([P, NB * PACK * D], BF16, name="r_sign")
                    nc.scalar.activation(out=r_sign[:], in_=r_flat[:, cols], func=ACT.Sign)
                    nc.scalar.activation(out=flat[:, cols], in_=r_sign[:], func=ACT.Relu)
            return mask

        def straight_backward(a):
            dr = work.tile([P, PACK, ROWS, PAIRS, 2], BF16, name="dr_straight")
            nc.vector.tensor_tensor(
                out=dr[:].rearrange("p j q i e -> p q j (i e)"),
                in0=mask_straight[a][:],
                in1=loaded_straight[a][1][:].rearrange("p b k (j d) -> p (b k) j d", j=PACK),
                op=ALU.mult,
            )
            return dr

        def straight_products(dr):
            products = []
            shape = [P, 2, PACK, ROWS, PAIRS]
            for channel in range(2):
                both = work.tile(shape, F32, name="both", bufs=4)
                nc.vector.tensor_tensor(
                    out=both[:],
                    in0=dr[:, :, :, :, channel].unsqueeze(1).to_broadcast(shape),
                    in1=table_planes[:, channel].unsqueeze(3).to_broadcast(shape),
                    op=ALU.mult,
                )
                products.append(both)
            return products

        def guard(products):
            pair = products[1][:, 0, 0, 0, 0:2]
            nc.vector.tensor_copy(out=pair, in_=pair)

        def combine(engine, parity, products):
            dy_plane = work.tile([P, ROWS * PAIRS, PACK], BF16, align_bytes=64, name="dy_plane_%d" % parity)
            engine.tensor_tensor(
                out=dy_plane[:].rearrange("p (c i) j -> p c j i", i=RUN),
                in0=products[parity][:, 0].rearrange("p j q (c i) -> p (q c) j i", i=RUN),
                in1=products[1 - parity][:, 1].rearrange("p j q (c i) -> p (q c) j i", i=RUN),
                op=(ALU.add if parity == 0 else ALU.subtract),
            )
            return dy_plane

        def sum_on_tensor(products):
            dy_plane = work.tile([P, ROWS * PAIRS, PACK], BF16, align_bytes=64, name="dy_plane_0")
            for row in range(0, ROWS, 2):
                plane_sum = psum.tile([P, PACK, 2, PAIRS], F32, name="summed", bufs=3)
                for t in range(2):
                    nc.tensor.matmul(
                        out=plane_sum[:].rearrange("p j q i -> p j (q i)"),
                        lhsT=ident_f[:],
                        rhs=products[t][:, t, :, row : row + 2].rearrange("p j q i -> p j (q i)"),
                        start=(t == 0),
                        stop=(t == 1),
                    )
                nc.scalar.copy(
                    out=dy_plane[:, row * PAIRS : (row + 2) * PAIRS],
                    in_=plane_sum[:].rearrange("p j q i -> p (q i) j"),
                )
            return dy_plane

        def quantise_plane(a, parity, dy_plane):
            plane_codes = keep.tile([P, NB * P], U32, align_bytes=64, name="plane_codes_%d_%d" % (a, parity))
            plane_scales = keep.tile([P, NB * P], U8, align_bytes=64, name="plane_scales_%d_%d" % (a, parity))
            nc.vector.quantize_mx(
                out=plane_codes[:].bitcast(E5M2_X4),
                scales=plane_scales[:],
                in_=dy_plane[:].rearrange("p c j -> p (c j)"),
            )
            g, first = straight[a]
            for k in range(NB):
                cols = slice(k * P, (k + 1) * P)
                plane_codes_of[(g, parity, first + k)] = (plane_codes[:, cols], plane_scales[:, cols])

        x_codes = keep.tile([P, B, C], U32, align_bytes=64)
        x_scales = keep.tile([P, B, C], U8, align_bytes=64)

        def regroup_x(chunk):
            x_grouped = work.tile([P, N_TILE, PACK], BF16, align_bytes=64, name="x_grouped", bufs=3)
            nc.scalar.copy(
                out=x_grouped[:].rearrange("p (c i) j -> p c j i", i=RUN),
                in_=x_rows[chunk][:].rearrange("p j (c i) -> p c j i", i=RUN),
            )
            return x_grouped

        def quantise_x(chunk):
            n, b = divmod(chunk, B)
            cols = slice(n * N_TILE, (n + 1) * N_TILE)
            nc.vector.quantize_mx(
                out=x_codes[:, b, cols].bitcast(E4M3_X4),
                scales=x_scales[:, b, cols],
                in_=x_grouped_of[chunk][:].rearrange("p c j -> p (c j)"),
            )

        def multiply(codes_for, n, acc, batches):
            for b in batches:
                dy_codes, dy_scales = codes_for(b)
                nc.tensor.matmul_mx(
                    out=acc[:],
                    lhsT=dy_codes.bitcast(E5M2_X4),
                    lhsT_scale=dy_scales,
                    rhs=x_codes[:, b, n * N_TILE : (n + 1) * N_TILE].bitcast(E4M3_X4),
                    rhs_scale=x_scales[:, b, n * N_TILE : (n + 1) * N_TILE],
                    start=(b == 0),
                    stop=(b == B - 1),
                )

        out_pairs = out.rearrange("(g m e) c -> g e m c", m=P, e=2)

        def store(rows_out, n, acc, engine_copy):
            out_rows = work.tile([P, N_TILE], F32, name="out_rows", bufs=4)
            engine_copy(out=out_rows[:], in_=acc[:])
            nc.scalar.dma_start(out=rows_out[:, n * N_TILE : (n + 1) * N_TILE], in_=out_rows[:])

        loaded = {}
        mask_of = {}
        dr_of = {}
        turned_of = {}
        products_of = {}
        grouped_of = {}
        codes_of = {}
        loaded_straight = {}
        mask_straight = {}
        both_of = {}
        even_plane = {}
        odd_plane = {}
        plane_codes_of = {}
        x_rows = {}
        x_grouped_of = {}

        load_order = [("r", k) for k in range(EARLY)]
        for k in range(max(n_pieces - EARLY, B * N_BANKS)):
            if k < B * N_BANKS:
                load_order.append(("x", k))
            if k + EARLY < n_pieces:
                load_order.append(("r", k + EARLY))
        load_order += [("s", a) for a in range(n_straight)]

        def issue(count):
            for kind, k in load_order[:count]:
                if kind == "r":
                    loaded[k] = load_piece(k)
                elif kind == "s":
                    loaded_straight[k] = load_straight(k)
                else:
                    x_rows[k] = load_x(k)
            return load_order[count:]

        table_rows = keep.tile([P, 2, PACK * D], BF16, name="table_rows")
        for t, source in enumerate((cos, sin)):
            nc.sync.dma_start(out=table_rows[:, t], in_=source.rearrange("(p j) d -> p (j d)", j=PACK))
        load_order = issue(6)

        ident_f = keep.tile([P, P], F32, name="ident_f")
        make_identity(nc, ident_f[:])
        ident_bf = keep.tile([P, P], BF16, name="ident_bf")
        nc.scalar.copy(out=ident_bf[:], in_=ident_f[:])
        swap_f = keep.tile([P, P], F32, name="swap_f")
        pairs_out = swap_f[:].rearrange("p (i e) -> p i e", e=2)
        pairs_in = ident_f[:].rearrange("p (i e) -> p i e", e=2)
        for e in range(2):
            nc.vector.tensor_copy(out=pairs_out[:, :, e], in_=pairs_in[:, :, 1 - e])

        tables = keep.tile([P, 2, PACK * P], BF16, name="tables")
        even_rows = keep.tile([P, 1], F32, name="even_rows")
        nc.vector.tensor_reduce(out=even_rows[:], in_=pairs_in[:, :, 0], op=ALU.add, axis=mybir.AxisListType.X)
        sign = keep.tile([P, 1], F32, name="sign")
        nc.vector.tensor_scalar(
            out=sign[:], in0=even_rows[:], scalar1=-2.0, scalar2=1.0, op0=ALU.mult, op1=ALU.add
        )
        turned_tables = turn(table_rows[:].rearrange("p t f -> p (t f)"))
        nc.scalar.copy(out=tables[:, 0], in_=turned_tables[:, : PACK * P])
        nc.scalar.activation(
            out=tables[:, 1], in_=turned_tables[:, PACK * P :], func=ACT.Copy, scale=sign[:]
        )
        table_planes = psum.tile([P, 2, 2, PACK, PAIRS], BF16, name="table_planes", bufs=1)

        def make_planes():
            for channel in range(2):
                for t in range(2):
                    nc.tensor.matmul(
                        out=table_planes[:, channel, t].rearrange("p j i -> p (j i)"),
                        lhsT=ident_bf[:],
                        rhs=table_rows[:, t].rearrange("p (q e) -> p q e", e=2)[:, :, channel],
                        start=True,
                        stop=True,
                    )

        waiting = []
        coming = []
        finished = []
        last_acc = {}
        x_done = 0
        x_step = {}
        for chunk in range(B * N_BANKS):
            x_step[chunk if chunk < X_FIRST else chunk + X_PAUSE] = chunk
        for step in range(-2, n_pieces + n_straight + 6):
            load_order = issue(3)
            a = step - n_pieces
            for k, (rows_out, n, acc) in enumerate(finished):
                on_vector = a > n_straight and k % 2 == 1
                store(rows_out, n, acc, nc.vector.tensor_copy if on_vector else nc.scalar.copy)
            finished = []
            if step in x_step:
                x_grouped_of[x_step[step]] = regroup_x(x_step[step])
            if a - 1 in PE_PIECES:
                even_plane[a - 1] = sum_on_tensor(both_of[a - 1])
            if 0 <= step < n_pieces:
                products_of[step] = rope_products(step, turned_of[step])
            if V_PRODUCTS <= step + 1 < n_pieces:
                multiply_mask(nc.vector, step + 1, dr_of[step + 1], slice(G_COLS, NB * PACK * D))
            if 0 <= a < n_straight:
                dr_straight = straight_backward(a)
            if 0 <= step - 1 < n_pieces:
                q = step - 1
                grouped_of[q] = work.tile([P, pieces[q][2], D, PACK], BF16, align_bytes=64, name="dy_grouped", bufs=3)
                for b in range(pieces[q][2]):
                    summed = add_back(products_of[q], b)
                    nc.scalar.copy(out=grouped_of[q][:, b], in_=summed[:].rearrange("p j d -> p d j"))
            if 0 <= step - 2 < n_pieces:
                quantise_piece(step - 2, grouped_of[step - 2])
            if step - X_LAG in x_step:
                quantise_x(x_step[step - X_LAG])
                x_done = x_step[step - X_LAG] + 1
            if 1 <= a <= n_straight:
                if a - 2 in PE_PIECES:
                    quantise_plane(a - 2, 1, odd_plane[a - 2])
                if a - 1 not in PE_PIECES:
                    quantise_plane(a - 1, 0, even_plane[a - 1])
                if a < n_straight:
                    guard(both_of[a - 1])
                odd_plane[a - 1] = combine(nc.gpsimd if a < n_straight else nc.vector, 1, both_of[a - 1])
            if 0 <= a < n_straight:
                both_of[a] = straight_products(dr_straight)
            if 0 <= a + 1 < min(n_straight, V_MASKS_A):
                mask_straight[a + 1] = straight_mask(a + 1)
            if 1 <= a <= n_straight:
                if a - 1 in PE_PIECES:
                    quantise_plane(a - 1, 0, even_plane[a - 1])
                else:
                    quantise_plane(a - 1, 1, odd_plane[a - 1])
            if 0 <= a < n_straight:
                if a not in PE_PIECES:
                    even_plane[a] = combine(nc.vector, 0, both_of[a])
            if 0 <= step + 2 < n_pieces:
                mask_of[step + 2] = relu_mask(step + 2)
                dr_of[step + 2] = relu_backward(step + 2)
            if V_MASKS_A <= a + MASK_LEAD < n_straight:
                mask_straight[a + MASK_LEAD] = straight_mask(a + MASK_LEAD)
            waiting += coming
            coming = []
            q = step - MX_LAG + 1
            if 0 <= q < n_pieces and pieces[q][1] + pieces[q][2] == B:
                h = pieces[q][0]
                for n in range(N_BANKS):
                    coming.append((n, out[h * D : (h + 1) * D], lambda b, h=h: codes_of[(h, b)]))
            limit = MX_LIMIT if step < n_pieces else 4
            ready = [item for item in waiting if x_done >= (item[0] + 1) * B][:limit]
            for item in ready:
                waiting.remove(item)
                acc = psum.tile([P, N_TILE], F32, name="acc")
                multiply(item[2], item[0], acc, range(B))
                finished.append((item[1], item[0], acc))
            if 1 <= a <= n_straight:
                g, first = straight[a - 1]
                if g < H // 2 - 1:
                    if first + NB == B:
                        for parity in range(2):
                            for n in range(N_BANKS):
                                coming.append(
                                    (n, out_pairs[g, parity], lambda b, g=g, e=parity: plane_codes_of[(g, e, b)])
                                )
                else:
                    for parity in range(2):
                        for n in range(N_BANKS):
                            if first == 0:
                                last_acc[(parity, n)] = psum.tile(
                                    [P, N_TILE], F32, name=("turned" if parity == 0 else "summed"),
                                    bufs=(2 if parity == 0 else 3),
                                )
                            multiply(
                                lambda b, g=g, e=parity: plane_codes_of[(g, e, b)],
                                n,
                                last_acc[(parity, n)],
                                range(first, first + NB),
                            )
                            if first + NB == B:
                                finished.append((out_pairs[g, parity], n, last_acc[(parity, n)]))
            if 0 <= step + 1 < n_pieces:
                turned_of[step + 1] = turn(dr_of[step + 1][:])
            if step == 1:
                make_planes()
